import numpy as np
import ml_dtypes


def mxq(x, axis, fmt="e4m3"):
    dtype, down = {"e4m3": (ml_dtypes.float8_e4m3fn, 7), "e5m2": (ml_dtypes.float8_e5m2, 14)}[fmt]
    v = np.moveaxis(np.asarray(x, np.float32).astype(ml_dtypes.bfloat16).astype(np.float64), axis, -1)
    blocks = v.reshape(v.shape[:-1] + (-1, 32))
    amax = np.abs(blocks).max(-1, keepdims=True)
    byte = np.maximum(np.where(amax > 0, np.frexp(amax)[1] - 1 + 127, 0) - down, 1)
    scale = np.exp2(byte - 127.0)
    codes = (blocks / scale).astype(np.float32).astype(dtype).astype(np.float64)
    return np.moveaxis((codes * scale).reshape(v.shape), -1, axis)


WIDE = False


def mx_kscale(k):
    if not WIDE:
        return np.ones(k)
    levels = np.array([10, -10, 5, -5, 0])
    a = np.random.permutation(np.resize(levels, k // 512 * 4)).reshape(k // 512, 4)
    idx = np.arange(k)
    return np.exp2(a[idx // 512, idx % 128 // 32])


BF16 = ml_dtypes.bfloat16


def bf(x):
    return np.asarray(x, np.float32).astype(BF16)


def f64(x):
    return np.asarray(x).astype(np.float64)


E2M1 = np.array([0.0, 0.5, 1.0, 1.5, 2.0, 3.0, 4.0, 6.0, -0.0, -0.5, -1.0, -1.5, -2.0, -3.0, -4.0, -6.0])


def pack_weight(w, fmt):
    k, n = w.shape
    w = f64(bf(w)).reshape(k // 32, 32, n)
    amax = np.abs(w).max(1)
    if fmt == "e4m3":
        byte = np.frexp(amax)[1] - 1 + 127 - 7
    else:
        mant, ex = np.frexp(amax / 6.0)
        byte = np.where(mant > 0.5, ex, ex - 1) + 127
    byte = np.clip(np.where(amax > 0, byte, 1), 1, 254)
    scaled = (w * np.exp2(127.0 - byte)[:, None, :]).reshape(k, n).astype(np.float32)
    by_word = np.ascontiguousarray(scaled.reshape(k // 512, 128, 4, n).transpose(0, 1, 3, 2))
    if fmt == "e4m3":
        words = by_word.astype(ml_dtypes.float8_e4m3fn).view(np.uint8)
    else:
        c = by_word.astype(ml_dtypes.float4_e2m1fn).view(np.uint8) & 0xF
        words = c[..., 0::2] | (c[..., 1::2] << 4)
    return np.ascontiguousarray(words), np.ascontiguousarray(byte.astype(np.uint8).reshape(k // 512, 16, n))


def unpack_weight(words, scales, fmt):
    g, p, n, _ = words.shape
    if fmt == "e4m3":
        vals = np.ascontiguousarray(words).view(ml_dtypes.float8_e4m3fn).astype(np.float64)
    else:
        nib = np.empty((g, p, n, 4), np.uint8)
        nib[..., 0::2] = words & 0xF
        nib[..., 1::2] = words >> 4
        vals = E2M1[nib]
    vals = vals * np.repeat(np.exp2(scales.astype(np.float64) - 127.0), 8, axis=1)[..., None]
    return vals.transpose(0, 1, 3, 2).reshape(g * 512, n)


B, CH, CQ, CV, H, W = 1, 1024, 128, 512, 32, 64
EPS = 1e-5
POOL = 2
HW = H * W
HW4 = HW // (POOL * POOL)
A = 1.5 / CQ ** 0.25
FMT = "e4m3"


def bn(y, s, b, m, v):
    inv = f64(s) / np.sqrt(f64(v) + EPS)
    return y * inv[None, :, None] + (f64(b) - f64(m) * inv)[None, :, None]


def maxpool(y):
    c = y.shape[1]
    return y.reshape(B, c, H // POOL, POOL, W // POOL, POOL).max(axis=(3, 5)).reshape(B, c, HW4)


def vec(c, z):
    return bf(z * np.random.standard_normal(c))


def pos(c):
    return bf(0.5 + np.random.random(c))


def setup_inputs():
    s = mx_kscale(CH)
    out = {'memory': bf(np.random.standard_normal((B, CH, H, W)) * s[None, :, None, None])}
    out['wq_words'], out['wq_scales'] = pack_weight((np.random.standard_normal((CQ, CH)) * A / np.sqrt(CH) / s).T, FMT)
    out.update({'bq': vec(CQ, 0.1),
                'bnq_s': pos(CQ), 'bnq_b': vec(CQ, 0.1), 'bnq_m': vec(CQ, 0.1), 'bnq_v': pos(CQ)})
    out['wk_words'], out['wk_scales'] = pack_weight((np.random.standard_normal((CQ, CH)) * A / np.sqrt(CH) / s).T, FMT)
    out.update({'bk': vec(CQ, 0.1),
                'bnk_s': pos(CQ), 'bnk_b': vec(CQ, 0.1), 'bnk_m': vec(CQ, 0.1), 'bnk_v': pos(CQ)})
    out['wv_words'], out['wv_scales'] = pack_weight((np.random.standard_normal((CV, CH)) / np.sqrt(CH) / s).T, FMT)
    out.update({'bv': vec(CV, 0.3),
                'bnv_s': pos(CV), 'bnv_b': vec(CV, 0.3), 'bnv_m': vec(CV, 0.3), 'bnv_v': pos(CV)})
    return out


def reference(memory, wq_words, wq_scales, bq, bnq_s, bnq_b, bnq_m, bnq_v, wk_words, wk_scales, bk, bnk_s, bnk_b, bnk_m, bnk_v, wv_words, wv_scales, bv, bnv_s, bnv_b, bnv_m, bnv_v):
    mq = mxq(f64(memory).reshape(B, CH, HW), 1, 'e4m3')
    yq = (unpack_weight(wq_words, wq_scales, FMT).T @ mq) + f64(bq)[None, :, None]
    yk = (unpack_weight(wk_words, wk_scales, FMT).T @ mq) + f64(bk)[None, :, None]
    yv = (unpack_weight(wv_words, wv_scales, FMT).T @ mq) + f64(bv)[None, :, None]
    q = bn(yq, bnq_s, bnq_b, bnq_m, bnq_v).transpose(0, 2, 1)
    k = maxpool(bn(yk, bnk_s, bnk_b, bnk_m, bnk_v))
    v = maxpool(bn(yv, bnv_s, bnv_b, bnv_m, bnv_v)).transpose(0, 2, 1)
    return q, k, v

@@ -1,0 +1,291 @@
+from contextlib import ExitStack
+
+import concourse.mybir as mybir
+from concourse.masks import make_identity
+
+F32 = mybir.dt.float32
+BF16 = mybir.dt.bfloat16
+I32 = mybir.dt.int32
+U32 = mybir.dt.uint32
+U8 = mybir.dt.uint8
+FP8X4 = mybir.dt.float8_e4m3fn_x4
+ALU = mybir.AluOpType
+ACT = mybir.ActivationFunctionType
+
+P = 128
+PACK = 4
+K_PASS = P * PACK
+CH, CQ, CV = 1024, 128, 512
+HEIGHT, WIDTH = 32, 64
+POSITIONS = HEIGHT * WIDTH
+EPS = 1e-5
+PASSES = CH // K_PASS
+CHUNK = 512
+N_CHUNKS = POSITIONS // CHUNK
+POOLED = CHUNK // 4
+V_TILES = CV // P
+QUADRANTS = 4
+RUN = 4
+VECTOR_COLS = 256
+V_LAG = 2
+QK_LAG = 4
+
+FLOPS = 2 * CH * POSITIONS * (CQ + CQ + CV)
+
+
+def load_weight(nc, keep, words_dram, scales_dram, n_out, name):
+    words = keep.tile([P, PASSES, n_out], U32, name=name + "_words", align_bytes=64)
+    nc.sync.dma_start(
+        out=words[:].bitcast(I32),
+        in_=words_dram.rearrange("g p n t -> p g (n t)").bitcast(I32),
+    )
+    planes = keep.tile([P, PASSES, n_out], U8, name=name + "_planes", align_bytes=64)
+    nc.vector.memset(planes[:].bitcast(I32), 0)
+    for quad in range(QUADRANTS):
+        nc.sync.dma_start(
+            out=planes[32 * quad : 32 * quad + 4].bitcast(I32),
+            in_=scales_dram[:, 4 * quad : 4 * quad + 4, :].rearrange("g r n -> r g n").bitcast(I32),
+        )
+    return words, planes
+
+
+def load_vectors(nc, keep, groups, name):
+    rows = keep.tile([P, P], BF16, name=name + "_rows")
+    nc.vector.memset(rows[:], 0.0)
+    row = 0
+    for vectors in groups:
+        for vector in vectors:
+            n_rows = vector.shape[0] // P
+            nc.sync.dma_start(out=rows[row : row + n_rows, :], in_=vector.rearrange("(m c) -> m c", c=P))
+            row += n_rows
+    return rows
+
+
+def batch_norm_columns(nc, keep, cols_psum, eps_col, n, name):
+    cols = keep.tile([P, 5, n], F32, name=name + "_cols")
+    nc.vector.tensor_copy(out=cols[:], in_=cols_psum[:, 0 : 5 * n].rearrange("p (i m) -> p i m", m=n))
+    bias, gain, shift, mean, variance = [cols[:, i, :] for i in range(5)]
+    inv = keep.tile([P, n], F32, name=name + "_inv")
+    offset = keep.tile([P, n], F32, name=name + "_offset")
+    nc.scalar.activation(out=inv[:], in_=variance, func=ACT.Sqrt, bias=eps_col[:], scale=1.0)
+    nc.vector.tensor_sub(out=offset[:], in0=bias, in1=mean)
+    nc.vector.reciprocal(out=inv[:], in_=inv[:])
+    nc.vector.tensor_mul(out=inv[:], in0=inv[:], in1=gain)
+    nc.vector.tensor_mul(out=offset[:], in0=offset[:], in1=inv[:])
+    nc.vector.tensor_add(out=offset[:], in0=offset[:], in1=shift)
+    return inv, offset
+
+
+def tile_selfattention_pa_kernel(
+    tc,
+    memory,
+    wq_words, wq_scales, bq, bnq_s, bnq_b, bnq_m, bnq_v,
+    wk_words, wk_scales, bk, bnk_s, bnk_b, bnk_m, bnk_v,
+    wv_words, wv_scales, bv, bnv_s, bnv_b, bnv_m, bnv_v,
+    out_0, out_1, out_2,
+):
+    nc = tc.nc
+    mem_rows = memory.rearrange("b (g p j) h w -> (b g) p j (h w)", p=P, j=PACK)
+
+    with ExitStack() as ctx:
+        keep = ctx.enter_context(tc.tile_pool(name="keep", bufs=1))
+        raw_pool = ctx.enter_context(tc.tile_pool(name="raw", bufs=N_CHUNKS * PASSES))
+        grouped_pool = ctx.enter_context(tc.tile_pool(name="grouped", bufs=4))
+        work = ctx.enter_context(tc.tile_pool(name="work", bufs=2))
+        halves = ctx.enter_context(tc.tile_pool(name="halves", bufs=4))
+        sums = ctx.enter_context(tc.psum_pool(name="sums", bufs=6))
+        turned = ctx.enter_context(tc.psum_pool(name="turned", bufs=2))
+        ctx.enter_context(tc.manual_schedule())
+
+        eps_col = keep.tile([P, 1], F32, name="eps_col")
+        nc.vector.memset(eps_col[:], EPS)
+        warm = keep.tile([P, 1], F32, name="warm")
+        nc.scalar.activation(out=warm[:], in_=eps_col[:], func=ACT.Sqrt)
+        identity = keep.tile([P, P], F32, name="identity")
+        make_identity(nc, identity[:])
+        identity_bf16 = keep.tile([P, P], BF16, name="identity_bf16")
+        make_identity(nc, identity_bf16[:])
+
+        raw = {}
+        for c in range(N_CHUNKS):
+            for g in range(PASSES):
+                raw[c, g] = raw_pool.tile([P, PACK, CHUNK], BF16, name="raw")
+                queue = nc.sync if (c, g) == (0, 0) else nc.gpsimd
+                queue.dma_start(out=raw[c, g][:], in_=mem_rows[g][:, :, c * CHUNK : (c + 1) * CHUNK])
+
+        wv, wv_planes = load_weight(nc, keep, wv_words, wv_scales, CV, "wv")
+        v_rows = load_vectors(nc, keep, ((bv,), (bnv_s,), (bnv_b,), (bnv_m,), (bnv_v,)), "v")
+        wq, wq_planes = load_weight(nc, keep, wq_words, wq_scales, CQ, "wq")
+        wk, wk_planes = load_weight(nc, keep, wk_words, wk_scales, CQ, "wk")
+        qk_rows = load_vectors(
+            nc, keep, ((bq, bk), (bnq_s, bnk_s), (bnq_b, bnk_b), (bnq_m, bnk_m), (bnq_v, bnk_v)), "qk"
+        )
+
+        mem_codes = keep.tile([P, N_CHUNKS, PASSES, CHUNK], U32, name="mem_codes", align_bytes=64)
+        mem_planes = keep.tile([P, N_CHUNKS, PASSES, CHUNK], U8, name="mem_planes", align_bytes=64)
+
+        def quantise_chunk(c):
+            grouped = {}
+            for g in range(PASSES):
+                grouped[g] = grouped_pool.tile([P, CHUNK, PACK], BF16, name="grouped", align_bytes=64)
+                for copy, cols in (
+                    (nc.vector.tensor_copy, slice(0, VECTOR_COLS)),
+                    (nc.scalar.copy, slice(VECTOR_COLS, CHUNK)),
+                ):
+                    copy(
+                        out=grouped[g][:, cols, :].rearrange("p (n i) j -> p n j i", i=RUN),
+                        in_=raw[c, g][:, :, cols].rearrange("p j (n i) -> p n j i", i=RUN),
+                    )
+            for g in range(PASSES):
+                nc.vector.quantize_mx(
+                    out=mem_codes[:, c, g, :].bitcast(FP8X4),
+                    scales=mem_planes[:, c, g, :],
+                    in_=grouped[g][:].rearrange("p n j -> p (n j)"),
+                )
+
+        def convolve(c, words, planes, channels):
+            acc = sums.tile([P, CHUNK], F32, name="acc")
+            for g in range(PASSES):
+                nc.tensor.matmul_mx(
+                    out=acc[:],
+                    lhsT=words[:, g, channels].bitcast(FP8X4),
+                    lhsT_scale=planes[:, g, channels],
+                    rhs=mem_codes[:, c, g, :].bitcast(FP8X4),
+                    rhs_scale=mem_planes[:, c, g, :],
+                    start=(g == 0),
+                    stop=(g == PASSES - 1),
+                )
+            return acc
+
+        def turn_vectors(rows, name):
+            cols_psum = turned.tile([P, P], BF16, tag="turned", name=name + "_cols_psum")
+            nc.tensor.transpose(cols_psum[:], rows[:], identity_bf16[:])
+            return cols_psum
+
+        def pool_rows(acc, inv_col, out):
+            by_row = acc[:].rearrange("ch (hp dh w) -> ch hp dh w", dh=2, w=WIDTH)
+            upper = halves.tile([P, CHUNK // 2], F32, name="upper")
+            upper_rows = upper[:].rearrange("ch (hp w) -> ch hp w", w=WIDTH)
+            nc.scalar.activation(out=upper_rows, in_=by_row[:, :, 0, :], func=ACT.Copy, scale=inv_col)
+            nc.vector.scalar_tensor_tensor(
+                out=out.rearrange("ch (hp w) -> ch hp w", w=WIDTH),
+                in0=by_row[:, :, 1, :],
+                scalar=inv_col,
+                in1=upper_rows,
+                op0=ALU.mult,
+                op1=ALU.max,
+            )
+
+        def pool_columns(tall, out):
+            pairs = tall.rearrange("ch (x dw) -> ch x dw", dw=2)
+            nc.vector.tensor_tensor(out=out, in0=pairs[:, :, 0], in1=pairs[:, :, 1], op=ALU.max)
+
+        v_acc, v_turned, q_acc, k_acc, q_turned = {}, {}, {}, {}, {}
+        norms, cols_psum = {}, {}
+        v_offset_rows = keep.tile([P, CV], F32, name="v_offset_rows")
+        k_pooled = keep.tile([P, N_CHUNKS * POOLED], F32, name="k_pooled")
+
+        def v_sums(c):
+            v_acc[c] = [convolve(c, wv, wv_planes, slice(m * P, (m + 1) * P)) for m in range(V_TILES)]
+
+        def spread_v_offset():
+            spread = turned.tile([P, CV], F32, tag="turned", name="spread")
+            for m in range(V_TILES):
+                nc.tensor.matmul(
+                    spread[:, m * P : (m + 1) * P],
+                    lhsT=norms["v"][1][:, m : m + 1].to_broadcast([P, P]),
+                    rhs=identity[:],
+                    start=True,
+                    stop=True,
+                )
+            nc.vector.tensor_copy(out=v_offset_rows[:], in_=spread[:])
+
+        def v_pool_and_turn(c):
+            inv = norms["v"][0]
+            tall = work.tile([P, V_TILES, CHUNK // 2], F32, name="tall")
+            for m in range(V_TILES):
+                pool_rows(v_acc[c][m], inv[:, m : m + 1], tall[:, m, :])
+            v_pooled = work.tile([P, V_TILES * POOLED], F32, name="v_pooled")
+            pool_columns(tall[:].rearrange("ch m x -> ch (m x)"), v_pooled[:])
+            v_turned[c] = turned.tile([P, CV], F32, tag="turned", name="v_turned")
+            for m in range(V_TILES):
+                block = slice(m * P, (m + 1) * P)
+                nc.tensor.transpose(v_turned[c][:, block], v_pooled[:, block], identity[:])
+
+        def v_store(c):
+            v_out = work.tile([P, CV], F32, name="v_out")
+            nc.vector.tensor_tensor(out=v_out[:], in0=v_turned[c][:], in1=v_offset_rows[:], op=ALU.add)
+            nc.sync.dma_start(out=out_2[0, c * POOLED : (c + 1) * POOLED, :], in_=v_out[:])
+
+        def qk_sums(c):
+            q_acc[c] = convolve(c, wq, wq_planes, slice(0, CQ))
+            k_acc[c] = convolve(c, wk, wk_planes, slice(0, CQ))
+
+        def q_norm_and_turn(c):
+            inv, offset = norms["qk"]
+            q_normed = work.tile([P, PACK, P], F32, name="q_normed")
+            nc.scalar.activation(
+                out=q_normed[:],
+                in_=q_acc[c][:].rearrange("ch (p i) -> ch i p", i=PACK),
+                func=ACT.Identity,
+                bias=offset[:, 0:1],
+                scale=inv[:, 0:1],
+            )
+            q_turned[c] = turned.tile([P, PACK, P], F32, tag="turned", name="q_turned")
+            for i in range(PACK):
+                nc.tensor.transpose(q_turned[c][:, i, :], q_normed[:, i, :], identity[:])
+
+        def k_pool(c):
+            k_tall = work.tile([P, CHUNK // 2], F32, name="k_tall")
+            pool_rows(k_acc[c], norms["qk"][0][:, 1:2], k_tall[:])
+            pool_columns(k_tall[:], k_pooled[:, c * POOLED : (c + 1) * POOLED])
+
+        def q_store(c):
+            q_out = work.tile([P, PACK, P], F32, name="q_out")
+            nc.scalar.copy(out=q_out[:], in_=q_turned[c][:])
+            nc.sync.dma_start(
+                out=out_0[0, c * CHUNK : (c + 1) * CHUNK, :].rearrange("(p i) ch -> p i ch", i=PACK),
+                in_=q_out[:],
+            )
+
+        def chunk_at(step, lag):
+            return step - lag if 0 <= step - lag < N_CHUNKS else None
+
+        for step in range(N_CHUNKS + QK_LAG + 1):
+            if step == V_LAG:
+                norms["v"] = batch_norm_columns(nc, keep, cols_psum["v"], eps_col, V_TILES, "v")
+            if step == QK_LAG:
+                norms["qk"] = batch_norm_columns(nc, keep, cols_psum["qk"], eps_col, 2, "qk")
+
+            c = chunk_at(step, V_LAG)
+            if c is not None:
+                v_pool_and_turn(c)
+            if step == V_LAG:
+                spread_v_offset()
+            c = chunk_at(step, 0)
+            if c is not None:
+                quantise_chunk(c)
+            if step == V_LAG - 1:
+                cols_psum["v"] = turn_vectors(v_rows, "v")
+            if step == QK_LAG - 1:
+                cols_psum["qk"] = turn_vectors(qk_rows, "qk")
+            c = chunk_at(step, 0)
+            if c is not None:
+                v_sums(c)
+            c = chunk_at(step, V_LAG + 1)
+            if c is not None:
+                v_store(c)
+            c = chunk_at(step, QK_LAG - 1)
+            if c is not None:
+                qk_sums(c)
+            c = chunk_at(step, QK_LAG)
+            if c is not None:
+                q_norm_and_turn(c)
+                k_pool(c)
+            c = chunk_at(step, QK_LAG + 1)
+            if c is not None:
+                q_store(c)
+
+        k_out = keep.tile([P, N_CHUNKS * POOLED], F32, name="k_out")
+        nc.vector.tensor_scalar_add(out=k_out[:], in0=k_pooled[:], scalar1=norms["qk"][1][:, 1:2])
+        nc.sync.dma_start(out=out_1[0], in_=k_out[:])

@@ -27,53 +27,38 @@ V_TILES = CV // P
 QUADRANTS = 4
 RUN = 4
 VECTOR_COLS = 256
-V_LAG = 2
-QK_LAG = 4
+AHEAD = 2
+FIRST_PIECES = 3
 
 FLOPS = 2 * CH * POSITIONS * (CQ + CQ + CV)
 
 
-def load_weight(nc, keep, words_dram, scales_dram, n_out, name):
+def weight_tiles(nc, keep, words_dram, scales_dram, n_out, name):
     words = keep.tile([P, PASSES, n_out], U32, name=name + "_words", align_bytes=64)
-    nc.sync.dma_start(
-        out=words[:].bitcast(I32),
-        in_=words_dram.rearrange("g p n t -> p g (n t)").bitcast(I32),
-    )
+    loads = [(words[:].bitcast(I32), words_dram.rearrange("g p n t -> p g (n t)").bitcast(I32))]
     planes = keep.tile([P, PASSES, n_out], U8, name=name + "_planes", align_bytes=64)
     nc.vector.memset(planes[:].bitcast(I32), 0)
     for quad in range(QUADRANTS):
-        nc.sync.dma_start(
-            out=planes[32 * quad : 32 * quad + 4].bitcast(I32),
-            in_=scales_dram[:, 4 * quad : 4 * quad + 4, :].rearrange("g r n -> r g n").bitcast(I32),
+        loads.append(
+            (
+                planes[32 * quad : 32 * quad + 4].bitcast(I32),
+                scales_dram[:, 4 * quad : 4 * quad + 4, :].rearrange("g r n -> r g n").bitcast(I32),
+            )
         )
-    return words, planes
+    return words, planes, loads
 
 
-def load_vectors(nc, keep, groups, name):
+def vector_rows(nc, keep, groups, name):
     rows = keep.tile([P, P], BF16, name=name + "_rows")
     nc.vector.memset(rows[:], 0.0)
+    loads = []
     row = 0
     for vectors in groups:
         for vector in vectors:
             n_rows = vector.shape[0] // P
-            nc.sync.dma_start(out=rows[row : row + n_rows, :], in_=vector.rearrange("(m c) -> m c", c=P))
+            loads.append((rows[row : row + n_rows, :], vector.rearrange("(m c) -> m c", c=P)))
             row += n_rows
-    return rows
-
-
-def batch_norm_columns(nc, keep, cols_psum, eps_col, n, name):
-    cols = keep.tile([P, 5, n], F32, name=name + "_cols")
-    nc.vector.tensor_copy(out=cols[:], in_=cols_psum[:, 0 : 5 * n].rearrange("p (i m) -> p i m", m=n))
-    bias, gain, shift, mean, variance = [cols[:, i, :] for i in range(5)]
-    inv = keep.tile([P, n], F32, name=name + "_inv")
-    offset = keep.tile([P, n], F32, name=name + "_offset")
-    nc.scalar.activation(out=inv[:], in_=variance, func=ACT.Sqrt, bias=eps_col[:], scale=1.0)
-    nc.vector.tensor_sub(out=offset[:], in0=bias, in1=mean)
-    nc.vector.reciprocal(out=inv[:], in_=inv[:])
-    nc.vector.tensor_mul(out=inv[:], in0=inv[:], in1=gain)
-    nc.vector.tensor_mul(out=offset[:], in0=offset[:], in1=inv[:])
-    nc.vector.tensor_add(out=offset[:], in0=offset[:], in1=shift)
-    return inv, offset
+    return rows, loads
 
 
 def tile_selfattention_pa_kernel(
@@ -99,27 +84,38 @@ def tile_selfattention_pa_kernel(
 
         eps_col = keep.tile([P, 1], F32, name="eps_col")
         nc.vector.memset(eps_col[:], EPS)
-        warm = keep.tile([P, 1], F32, name="warm")
-        nc.scalar.activation(out=warm[:], in_=eps_col[:], func=ACT.Sqrt)
-        identity = keep.tile([P, P], F32, name="identity")
-        make_identity(nc, identity[:])
-        identity_bf16 = keep.tile([P, P], BF16, name="identity_bf16")
-        make_identity(nc, identity_bf16[:])
 
-        raw = {}
-        for c in range(N_CHUNKS):
-            for g in range(PASSES):
-                raw[c, g] = raw_pool.tile([P, PACK, CHUNK], BF16, name="raw")
-                queue = nc.sync if (c, g) == (0, 0) else nc.gpsimd
-                queue.dma_start(out=raw[c, g][:], in_=mem_rows[g][:, :, c * CHUNK : (c + 1) * CHUNK])
-
-        wv, wv_planes = load_weight(nc, keep, wv_words, wv_scales, CV, "wv")
-        v_rows = load_vectors(nc, keep, ((bv,), (bnv_s,), (bnv_b,), (bnv_m,), (bnv_v,)), "v")
-        wq, wq_planes = load_weight(nc, keep, wq_words, wq_scales, CQ, "wq")
-        wk, wk_planes = load_weight(nc, keep, wk_words, wk_scales, CQ, "wk")
-        qk_rows = load_vectors(
+        wv, wv_planes, wv_loads = weight_tiles(nc, keep, wv_words, wv_scales, CV, "wv")
+        wq, wq_planes, wq_loads = weight_tiles(nc, keep, wq_words, wq_scales, CQ, "wq")
+        wk, wk_planes, wk_loads = weight_tiles(nc, keep, wk_words, wk_scales, CQ, "wk")
+        v_rows, v_row_loads = vector_rows(nc, keep, ((bv,), (bnv_s,), (bnv_b,), (bnv_m,), (bnv_v,)), "v")
+        qk_rows, qk_row_loads = vector_rows(
             nc, keep, ((bq, bk), (bnq_s, bnk_s), (bnq_b, bnk_b), (bnq_m, bnk_m), (bnq_v, bnk_v)), "qk"
         )
+        pieces = [(c, g) for c in range(N_CHUNKS) for g in range(PASSES)]
+        raw = {}
+
+        def load_pieces(queue, some_pieces):
+            for c, g in some_pieces:
+                raw[c, g] = raw_pool.tile([P, PACK, CHUNK], BF16, name="raw")
+                queue.dma_start(out=raw[c, g][:], in_=mem_rows[g][:, :, c * CHUNK : (c + 1) * CHUNK])
+
+        def load_small(queue, loads):
+            for out, in_ in loads:
+                queue.dma_start(out=out, in_=in_)
+
+        load_small(nc.gpsimd, v_row_loads)
+        load_small(nc.sync, wv_loads)
+        load_pieces(nc.scalar, pieces[:FIRST_PIECES])
+        load_pieces(nc.sync, pieces[FIRST_PIECES:])
+        load_small(nc.sync, wq_loads + wk_loads + qk_row_loads)
+
+        warm = keep.tile([P, 1], F32, name="warm")
+        nc.scalar.activation(out=warm[:], in_=eps_col[:], func=ACT.Sqrt)
+        identity_bf16 = keep.tile([P, P], BF16, name="identity_bf16")
+        make_identity(nc, identity_bf16[:])
+        identity = keep.tile([P, P], F32, name="identity")
+        make_identity(nc, identity[:])
 
         mem_codes = keep.tile([P, N_CHUNKS, PASSES, CHUNK], U32, name="mem_codes", align_bytes=64)
         mem_planes = keep.tile([P, N_CHUNKS, PASSES, CHUNK], U8, name="mem_planes", align_bytes=64)
@@ -157,10 +153,21 @@ def tile_selfattention_pa_kernel(
                 )
             return acc
 
-        def turn_vectors(rows, name):
+        def batch_norm_columns(rows, n, name):
             cols_psum = turned.tile([P, P], BF16, tag="turned", name=name + "_cols_psum")
             nc.tensor.transpose(cols_psum[:], rows[:], identity_bf16[:])
-            return cols_psum
+            cols = keep.tile([P, 5, n], F32, name=name + "_cols")
+            nc.vector.tensor_copy(out=cols[:], in_=cols_psum[:, 0 : 5 * n].rearrange("p (i m) -> p i m", m=n))
+            bias, gain, shift, mean, variance = [cols[:, i, :] for i in range(5)]
+            inv = keep.tile([P, n], F32, name=name + "_inv")
+            offset = keep.tile([P, n], F32, name=name + "_offset")
+            nc.scalar.activation(out=inv[:], in_=variance, func=ACT.Sqrt, bias=eps_col[:], scale=1.0)
+            nc.vector.tensor_sub(out=offset[:], in0=bias, in1=mean)
+            nc.vector.reciprocal(out=inv[:], in_=inv[:])
+            nc.vector.tensor_mul(out=inv[:], in0=inv[:], in1=gain)
+            nc.vector.tensor_mul(out=offset[:], in0=offset[:], in1=inv[:])
+            nc.vector.tensor_add(out=offset[:], in0=offset[:], in1=shift)
+            return inv, offset
 
         def pool_rows(acc, inv_col, out):
             by_row = acc[:].rearrange("ch (hp dh w) -> ch hp dh w", dh=2, w=WIDTH)
@@ -180,37 +187,31 @@ def tile_selfattention_pa_kernel(
             pairs = tall.rearrange("ch (x dw) -> ch x dw", dw=2)
             nc.vector.tensor_tensor(out=out, in0=pairs[:, :, 0], in1=pairs[:, :, 1], op=ALU.max)
 
-        v_acc, v_turned, q_acc, k_acc, q_turned = {}, {}, {}, {}, {}
-        norms, cols_psum = {}, {}
-        v_offset_rows = keep.tile([P, CV], F32, name="v_offset_rows")
+        v_acc, v_pooled, v_turned, q_acc, k_acc, q_normed, q_turned = {}, {}, {}, {}, {}, {}, {}
+        norms = {}
         k_pooled = keep.tile([P, N_CHUNKS * POOLED], F32, name="k_pooled")
 
         def v_sums(c):
             v_acc[c] = [convolve(c, wv, wv_planes, slice(m * P, (m + 1) * P)) for m in range(V_TILES)]
 
-        def spread_v_offset():
-            spread = turned.tile([P, CV], F32, tag="turned", name="spread")
-            for m in range(V_TILES):
-                nc.tensor.matmul(
-                    spread[:, m * P : (m + 1) * P],
-                    lhsT=norms["v"][1][:, m : m + 1].to_broadcast([P, P]),
-                    rhs=identity[:],
-                    start=True,
-                    stop=True,
-                )
-            nc.vector.tensor_copy(out=v_offset_rows[:], in_=spread[:])
-
-        def v_pool_and_turn(c):
+        def v_leave(c):
             inv = norms["v"][0]
             tall = work.tile([P, V_TILES, CHUNK // 2], F32, name="tall")
             for m in range(V_TILES):
                 pool_rows(v_acc[c][m], inv[:, m : m + 1], tall[:, m, :])
-            v_pooled = work.tile([P, V_TILES * POOLED], F32, name="v_pooled")
-            pool_columns(tall[:].rearrange("ch m x -> ch (m x)"), v_pooled[:])
+            v_pooled[c] = work.tile([P, V_TILES * POOLED], F32, name="v_pooled")
+            pool_columns(tall[:].rearrange("ch m x -> ch (m x)"), v_pooled[c][:])
+
+        def v_turn(c):
+            if c == 0:
+                spread = turned.tile([P, CV], F32, tag="turned", name="spread")
+                for m in range(V_TILES):
+                    nc.tensor.transpose(spread[:, m * P : (m + 1) * P], v_offset_cols[:, m, :], identity[:])
+                nc.vector.tensor_copy(out=v_offset_rows[:], in_=spread[:])
             v_turned[c] = turned.tile([P, CV], F32, tag="turned", name="v_turned")
             for m in range(V_TILES):
                 block = slice(m * P, (m + 1) * P)
-                nc.tensor.transpose(v_turned[c][:, block], v_pooled[:, block], identity[:])
+                nc.tensor.transpose(v_turned[c][:, block], v_pooled[c][:, block], identity[:])
 
         def v_store(c):
             v_out = work.tile([P, CV], F32, name="v_out")
@@ -221,24 +222,24 @@ def tile_selfattention_pa_kernel(
             q_acc[c] = convolve(c, wq, wq_planes, slice(0, CQ))
             k_acc[c] = convolve(c, wk, wk_planes, slice(0, CQ))
 
-        def q_norm_and_turn(c):
+        def qk_leave(c):
             inv, offset = norms["qk"]
-            q_normed = work.tile([P, PACK, P], F32, name="q_normed")
+            q_normed[c] = work.tile([P, PACK, P], F32, name="q_normed")
             nc.scalar.activation(
-                out=q_normed[:],
+                out=q_normed[c][:],
                 in_=q_acc[c][:].rearrange("ch (p i) -> ch i p", i=PACK),
                 func=ACT.Identity,
                 bias=offset[:, 0:1],
                 scale=inv[:, 0:1],
             )
+            k_tall = work.tile([P, CHUNK // 2], F32, name="k_tall")
+            pool_rows(k_acc[c], inv[:, 1:2], k_tall[:])
+            pool_columns(k_tall[:], k_pooled[:, c * POOLED : (c + 1) * POOLED])
+
+        def q_turn(c):
             q_turned[c] = turned.tile([P, PACK, P], F32, tag="turned", name="q_turned")
             for i in range(PACK):
-                nc.tensor.transpose(q_turned[c][:, i, :], q_normed[:, i, :], identity[:])
-
-        def k_pool(c):
-            k_tall = work.tile([P, CHUNK // 2], F32, name="k_tall")
-            pool_rows(k_acc[c], norms["qk"][0][:, 1:2], k_tall[:])
-            pool_columns(k_tall[:], k_pooled[:, c * POOLED : (c + 1) * POOLED])
+                nc.tensor.transpose(q_turned[c][:, i, :], q_normed[c][:, i, :], identity[:])
 
         def q_store(c):
             q_out = work.tile([P, PACK, P], F32, name="q_out")
@@ -248,43 +249,38 @@ def tile_selfattention_pa_kernel(
                 in_=q_out[:],
             )
 
-        def chunk_at(step, lag):
-            return step - lag if 0 <= step - lag < N_CHUNKS else None
+        v_stages = (v_sums, v_leave, v_turn, v_store)
+        qk_stages = (qk_sums, qk_leave, q_turn, q_store)
+        jobs = []
+        for c in range(N_CHUNKS + 1):
+            if c < N_CHUNKS:
+                jobs.append((v_stages, c))
+            if c >= 1:
+                jobs.append((qk_stages, c - 1))
 
-        for step in range(N_CHUNKS + QK_LAG + 1):
-            if step == V_LAG:
-                norms["v"] = batch_norm_columns(nc, keep, cols_psum["v"], eps_col, V_TILES, "v")
-            if step == QK_LAG:
-                norms["qk"] = batch_norm_columns(nc, keep, cols_psum["qk"], eps_col, 2, "qk")
-
-            c = chunk_at(step, V_LAG)
-            if c is not None:
-                v_pool_and_turn(c)
-            if step == V_LAG:
-                spread_v_offset()
-            c = chunk_at(step, 0)
-            if c is not None:
-                quantise_chunk(c)
-            if step == V_LAG - 1:
-                cols_psum["v"] = turn_vectors(v_rows, "v")
-            if step == QK_LAG - 1:
-                cols_psum["qk"] = turn_vectors(qk_rows, "qk")
-            c = chunk_at(step, 0)
-            if c is not None:
-                v_sums(c)
-            c = chunk_at(step, V_LAG + 1)
-            if c is not None:
-                v_store(c)
-            c = chunk_at(step, QK_LAG - 1)
-            if c is not None:
-                qk_sums(c)
-            c = chunk_at(step, QK_LAG)
-            if c is not None:
-                q_norm_and_turn(c)
-                k_pool(c)
-            c = chunk_at(step, QK_LAG + 1)
-            if c is not None:
-                q_store(c)
+        quantise_chunk(0)
+        v_sums(0)
+        quantise_chunk(1)
+        norms["v"] = batch_norm_columns(v_rows, V_TILES, "v")
+        v_offset_cols = keep.tile([P, V_TILES, P], F32, name="v_offset_cols")
+        nc.vector.tensor_copy(out=v_offset_cols[:], in_=norms["v"][1][:].unsqueeze(2).to_broadcast([P, V_TILES, P]))
+        v_offset_rows = keep.tile([P, CV], F32, name="v_offset_rows")
+        v_sums(1)
+        for i, (stages, c) in enumerate(jobs):
+            start_sums, leave, turn, store = stages
+            leave(c)
+            if stages is v_stages and c + AHEAD < N_CHUNKS:
+                quantise_chunk(c + AHEAD)
+            turn(c)
+            for later_stages, later_c in jobs[i + AHEAD : i + AHEAD + 1]:
+                later_stages[0](later_c)
+            if i >= 1:
+                earlier_stages, earlier_c = jobs[i - 1]
+                earlier_stages[3](earlier_c)
+            if jobs[i + 1 : i + 2] == [(qk_stages, 0)]:
+                norms["qk"] = batch_norm_columns(qk_rows, 2, "qk")
+        last_stages, last_c = jobs[-1]
+        last_stages[3](last_c)
 
         k_out = keep.tile([P, N_CHUNKS * POOLED], F32, name="k_out")
         nc.vector.tensor_scalar_add(out=k_out[:], in0=k_pooled[:], scalar1=norms["qk"][1][:, 1:2])

@@ -28,7 +28,7 @@ QUADRANTS = 4
 RUN = 4
 VECTOR_COLS = 256
 AHEAD = 2
-FIRST_PIECES = 3
+FIRST_PIECES = 5
 
 FLOPS = 2 * CH * POSITIONS * (CQ + CQ + CV)
 
@@ -80,7 +80,6 @@ def tile_selfattention_pa_kernel(
         halves = ctx.enter_context(tc.tile_pool(name="halves", bufs=4))
         sums = ctx.enter_context(tc.psum_pool(name="sums", bufs=6))
         turned = ctx.enter_context(tc.psum_pool(name="turned", bufs=2))
-        ctx.enter_context(tc.manual_schedule())
 
         eps_col = keep.tile([P, 1], F32, name="eps_col")
         nc.vector.memset(eps_col[:], EPS)
@@ -104,9 +103,9 @@ def tile_selfattention_pa_kernel(
             for out, in_ in loads:
                 queue.dma_start(out=out, in_=in_)
 
-        load_small(nc.gpsimd, v_row_loads)
         load_small(nc.sync, wv_loads)
-        load_pieces(nc.scalar, pieces[:FIRST_PIECES])
+        load_pieces(nc.sync, pieces[:FIRST_PIECES])
+        load_small(nc.sync, v_row_loads)
         load_pieces(nc.sync, pieces[FIRST_PIECES:])
         load_small(nc.sync, wq_loads + wk_loads + qk_row_loads)
 

@@ -28,7 +28,7 @@ QUADRANTS = 4
 RUN = 4
 VECTOR_COLS = 256
 AHEAD = 2
-FIRST_PIECES = 5
+FIRST_PIECES = 4
 
 FLOPS = 2 * CH * POSITIONS * (CQ + CQ + CV)
 
@@ -84,13 +84,13 @@ def tile_selfattention_pa_kernel(
         eps_col = keep.tile([P, 1], F32, name="eps_col")
         nc.vector.memset(eps_col[:], EPS)
 
-        wv, wv_planes, wv_loads = weight_tiles(nc, keep, wv_words, wv_scales, CV, "wv")
-        wq, wq_planes, wq_loads = weight_tiles(nc, keep, wq_words, wq_scales, CQ, "wq")
-        wk, wk_planes, wk_loads = weight_tiles(nc, keep, wk_words, wk_scales, CQ, "wk")
         v_rows, v_row_loads = vector_rows(nc, keep, ((bv,), (bnv_s,), (bnv_b,), (bnv_m,), (bnv_v,)), "v")
         qk_rows, qk_row_loads = vector_rows(
             nc, keep, ((bq, bk), (bnq_s, bnk_s), (bnq_b, bnk_b), (bnq_m, bnk_m), (bnq_v, bnk_v)), "qk"
         )
+        wv, wv_planes, wv_loads = weight_tiles(nc, keep, wv_words, wv_scales, CV, "wv")
+        wq, wq_planes, wq_loads = weight_tiles(nc, keep, wq_words, wq_scales, CQ, "wq")
+        wk, wk_planes, wk_loads = weight_tiles(nc, keep, wk_words, wk_scales, CQ, "wk")
         pieces = [(c, g) for c in range(N_CHUNKS) for g in range(PASSES)]
         raw = {}
 
@@ -103,11 +103,11 @@ def tile_selfattention_pa_kernel(
             for out, in_ in loads:
                 queue.dma_start(out=out, in_=in_)
 
+        load_small(nc.scalar, v_row_loads + qk_row_loads)
         load_small(nc.sync, wv_loads)
         load_pieces(nc.sync, pieces[:FIRST_PIECES])
-        load_small(nc.sync, v_row_loads)
+        load_small(nc.sync, wq_loads + wk_loads)
         load_pieces(nc.sync, pieces[FIRST_PIECES:])
-        load_small(nc.sync, wq_loads + wk_loads + qk_row_loads)
 
         warm = keep.tile([P, 1], F32, name="warm")
         nc.scalar.activation(out=warm[:], in_=eps_col[:], func=ACT.Sqrt)
@@ -202,11 +202,6 @@ def tile_selfattention_pa_kernel(
             pool_columns(tall[:].rearrange("ch m x -> ch (m x)"), v_pooled[c][:])
 
         def v_turn(c):
-            if c == 0:
-                spread = turned.tile([P, CV], F32, tag="turned", name="spread")
-                for m in range(V_TILES):
-                    nc.tensor.transpose(spread[:, m * P : (m + 1) * P], v_offset_cols[:, m, :], identity[:])
-                nc.vector.tensor_copy(out=v_offset_rows[:], in_=spread[:])
             v_turned[c] = turned.tile([P, CV], F32, tag="turned", name="v_turned")
             for m in range(V_TILES):
                 block = slice(m * P, (m + 1) * P)
@@ -257,13 +252,19 @@ def tile_selfattention_pa_kernel(
             if c >= 1:
                 jobs.append((qk_stages, c - 1))
 
-        quantise_chunk(0)
-        v_sums(0)
-        quantise_chunk(1)
         norms["v"] = batch_norm_columns(v_rows, V_TILES, "v")
+        norms["qk"] = batch_norm_columns(qk_rows, 2, "qk")
         v_offset_cols = keep.tile([P, V_TILES, P], F32, name="v_offset_cols")
         nc.vector.tensor_copy(out=v_offset_cols[:], in_=norms["v"][1][:].unsqueeze(2).to_broadcast([P, V_TILES, P]))
         v_offset_rows = keep.tile([P, CV], F32, name="v_offset_rows")
+        spread = turned.tile([P, CV], F32, tag="turned", name="spread")
+        for m in range(V_TILES):
+            nc.tensor.transpose(spread[:, m * P : (m + 1) * P], v_offset_cols[:, m, :], identity[:])
+        nc.vector.tensor_copy(out=v_offset_rows[:], in_=spread[:])
+
+        quantise_chunk(0)
+        v_sums(0)
+        quantise_chunk(1)
         v_sums(1)
         for i, (stages, c) in enumerate(jobs):
             start_sums, leave, turn, store = stages
@@ -276,8 +277,6 @@ def tile_selfattention_pa_kernel(
             if i >= 1:
                 earlier_stages, earlier_c = jobs[i - 1]
                 earlier_stages[3](earlier_c)
-            if jobs[i + 1 : i + 2] == [(qk_stages, 0)]:
-                norms["qk"] = batch_norm_columns(qk_rows, 2, "qk")
         last_stages, last_c = jobs[-1]
         last_stages[3](last_c)
 

@@ -28,7 +28,10 @@ QUADRANTS = 4
 RUN = 4
 VECTOR_COLS = 256
 AHEAD = 2
-FIRST_PIECES = 4
+BANKS = 6
+LEAD = 2
+V_NAMES = ("v0", "v1", "v2", "v3")
+JOBS = (("v", 0), ("v", 1), ("q", 0), ("v", 2), ("q", 1), ("v", 3), ("q", 2), ("q", 3))
 
 FLOPS = 2 * CH * POSITIONS * (CQ + CQ + CV)
 
@@ -50,7 +53,7 @@ def weight_tiles(nc, keep, words_dram, scales_dram, n_out, name):
 
 def vector_rows(nc, keep, groups, name):
     rows = keep.tile([P, P], BF16, name=name + "_rows")
-    nc.vector.memset(rows[:], 0.0)
+    nc.gpsimd.memset(rows[:], 0.0)
     loads = []
     row = 0
     for vectors in groups:
@@ -80,6 +83,7 @@ def tile_selfattention_pa_kernel(
         halves = ctx.enter_context(tc.tile_pool(name="halves", bufs=4))
         sums = ctx.enter_context(tc.psum_pool(name="sums", bufs=6))
         turned = ctx.enter_context(tc.psum_pool(name="turned", bufs=2))
+        ctx.enter_context(tc.manual_schedule())
 
         eps_col = keep.tile([P, 1], F32, name="eps_col")
         nc.vector.memset(eps_col[:], EPS)
@@ -91,23 +95,28 @@ def tile_selfattention_pa_kernel(
         wv, wv_planes, wv_loads = weight_tiles(nc, keep, wv_words, wv_scales, CV, "wv")
         wq, wq_planes, wq_loads = weight_tiles(nc, keep, wq_words, wq_scales, CQ, "wq")
         wk, wk_planes, wk_loads = weight_tiles(nc, keep, wk_words, wk_scales, CQ, "wk")
-        pieces = [(c, g) for c in range(N_CHUNKS) for g in range(PASSES)]
         raw = {}
 
-        def load_pieces(queue, some_pieces):
-            for c, g in some_pieces:
-                raw[c, g] = raw_pool.tile([P, PACK, CHUNK], BF16, name="raw")
-                queue.dma_start(out=raw[c, g][:], in_=mem_rows[g][:, :, c * CHUNK : (c + 1) * CHUNK])
+        def load_piece(c, g):
+            raw[c, g] = raw_pool.tile([P, PACK, CHUNK], BF16, name="raw")
+            nc.sync.dma_start(out=raw[c, g][:], in_=mem_rows[g][:, :, c * CHUNK : (c + 1) * CHUNK])
 
-        def load_small(queue, loads):
+        def load_small(loads):
             for out, in_ in loads:
-                queue.dma_start(out=out, in_=in_)
+                nc.sync.dma_start(out=out, in_=in_)
 
-        load_small(nc.scalar, v_row_loads + qk_row_loads)
-        load_small(nc.sync, wv_loads)
-        load_pieces(nc.sync, pieces[:FIRST_PIECES])
-        load_small(nc.sync, wq_loads + wk_loads)
-        load_pieces(nc.sync, pieces[FIRST_PIECES:])
+        load_piece(0, 0)
+        load_small(v_row_loads)
+        load_piece(0, 1)
+        load_small(wv_loads)
+        load_piece(1, 0)
+        load_piece(1, 1)
+        load_small(qk_row_loads)
+        load_piece(2, 0)
+        load_piece(2, 1)
+        load_small(wq_loads[:1] + wk_loads[:1] + wq_loads[1:] + wk_loads[1:])
+        load_piece(3, 0)
+        load_piece(3, 1)
 
         warm = keep.tile([P, 1], F32, name="warm")
         nc.scalar.activation(out=warm[:], in_=eps_col[:], func=ACT.Sqrt)
@@ -118,31 +127,41 @@ def tile_selfattention_pa_kernel(
 
         mem_codes = keep.tile([P, N_CHUNKS, PASSES, CHUNK], U32, name="mem_codes", align_bytes=64)
         mem_planes = keep.tile([P, N_CHUNKS, PASSES, CHUNK], U8, name="mem_planes", align_bytes=64)
+        grouped = {}
 
-        def quantise_chunk(c):
-            grouped = {}
-            for g in range(PASSES):
-                grouped[g] = grouped_pool.tile([P, CHUNK, PACK], BF16, name="grouped", align_bytes=64)
-                for copy, cols in (
-                    (nc.vector.tensor_copy, slice(0, VECTOR_COLS)),
-                    (nc.scalar.copy, slice(VECTOR_COLS, CHUNK)),
-                ):
-                    copy(
-                        out=grouped[g][:, cols, :].rearrange("p (n i) j -> p n j i", i=RUN),
-                        in_=raw[c, g][:, :, cols].rearrange("p j (n i) -> p n j i", i=RUN),
-                    )
-            for g in range(PASSES):
-                nc.vector.quantize_mx(
-                    out=mem_codes[:, c, g, :].bitcast(FP8X4),
-                    scales=mem_planes[:, c, g, :],
-                    in_=grouped[g][:].rearrange("p n j -> p (n j)"),
-                )
+        def regroup(copy, cols, c, g):
+            if (c, g) not in grouped:
+                grouped[c, g] = grouped_pool.tile([P, CHUNK, PACK], BF16, name="grouped", align_bytes=64)
+            copy(
+                out=grouped[c, g][:, cols, :].rearrange("p (n i) j -> p n j i", i=RUN),
+                in_=raw[c, g][:, :, cols].rearrange("p j (n i) -> p n j i", i=RUN),
+            )
 
-        def convolve(c, words, planes, channels):
-            acc = sums.tile([P, CHUNK], F32, name="acc")
-            for g in range(PASSES):
+        def regroup_vector(c, g):
+            regroup(nc.vector.tensor_copy, slice(0, VECTOR_COLS), c, g)
+
+        def regroup_scalar(c, g):
+            regroup(nc.scalar.copy, slice(VECTOR_COLS, CHUNK), c, g)
+
+        def quantise(c, g):
+            nc.vector.quantize_mx(
+                out=mem_codes[:, c, g, :].bitcast(FP8X4),
+                scales=mem_planes[:, c, g, :],
+                in_=grouped[c, g][:].rearrange("p n j -> p (n j)"),
+            )
+
+        weights = {"q": (wq, wq_planes, slice(0, CQ)), "k": (wk, wk_planes, slice(0, CQ))}
+        for m in range(V_TILES):
+            weights["v%d" % m] = (wv, wv_planes, slice(m * P, (m + 1) * P))
+        acc = {}
+
+        def multiply(c, name, passes):
+            if (c, name) not in acc:
+                acc[c, name] = sums.tile([P, CHUNK], F32, name="acc")
+            words, planes, channels = weights[name]
+            for g in passes:
                 nc.tensor.matmul_mx(
-                    out=acc[:],
+                    out=acc[c, name][:],
                     lhsT=words[:, g, channels].bitcast(FP8X4),
                     lhsT_scale=planes[:, g, channels],
                     rhs=mem_codes[:, c, g, :].bitcast(FP8X4),
@@ -150,56 +169,83 @@ def tile_selfattention_pa_kernel(
                     start=(g == 0),
                     stop=(g == PASSES - 1),
                 )
-            return acc
 
-        def batch_norm_columns(rows, n, name):
+        cols, inv, offset = {}, {}, {}
+
+        def norm_turn(rows, n, name):
             cols_psum = turned.tile([P, P], BF16, tag="turned", name=name + "_cols_psum")
             nc.tensor.transpose(cols_psum[:], rows[:], identity_bf16[:])
-            cols = keep.tile([P, 5, n], F32, name=name + "_cols")
-            nc.vector.tensor_copy(out=cols[:], in_=cols_psum[:, 0 : 5 * n].rearrange("p (i m) -> p i m", m=n))
-            bias, gain, shift, mean, variance = [cols[:, i, :] for i in range(5)]
-            inv = keep.tile([P, n], F32, name=name + "_inv")
-            offset = keep.tile([P, n], F32, name=name + "_offset")
-            nc.scalar.activation(out=inv[:], in_=variance, func=ACT.Sqrt, bias=eps_col[:], scale=1.0)
-            nc.vector.tensor_sub(out=offset[:], in0=bias, in1=mean)
-            nc.vector.reciprocal(out=inv[:], in_=inv[:])
-            nc.vector.tensor_mul(out=inv[:], in0=inv[:], in1=gain)
-            nc.vector.tensor_mul(out=offset[:], in0=offset[:], in1=inv[:])
-            nc.vector.tensor_add(out=offset[:], in0=offset[:], in1=shift)
-            return inv, offset
+            cols[name] = keep.tile([P, 5, n], F32, name=name + "_cols")
+            nc.vector.tensor_copy(out=cols[name][:], in_=cols_psum[:, 0 : 5 * n].rearrange("p (i m) -> p i m", m=n))
+            inv[name] = keep.tile([P, n], F32, name=name + "_inv")
+            offset[name] = keep.tile([P, n], F32, name=name + "_offset")
+            nc.vector.tensor_sub(out=offset[name][:], in0=cols[name][:, 0, :], in1=cols[name][:, 3, :])
 
-        def pool_rows(acc, inv_col, out):
-            by_row = acc[:].rearrange("ch (hp dh w) -> ch hp dh w", dh=2, w=WIDTH)
-            upper = halves.tile([P, CHUNK // 2], F32, name="upper")
-            upper_rows = upper[:].rearrange("ch (hp w) -> ch hp w", w=WIDTH)
-            nc.scalar.activation(out=upper_rows, in_=by_row[:, :, 0, :], func=ACT.Copy, scale=inv_col)
+        def norm_root(name):
+            nc.scalar.activation(out=inv[name][:], in_=cols[name][:, 4, :], func=ACT.Sqrt, bias=eps_col[:], scale=1.0)
+
+        def norm_finish(name):
+            nc.vector.reciprocal(out=inv[name][:], in_=inv[name][:])
+            nc.vector.tensor_mul(out=inv[name][:], in0=inv[name][:], in1=cols[name][:, 1, :])
+            nc.vector.tensor_mul(out=offset[name][:], in0=offset[name][:], in1=inv[name][:])
+            nc.vector.tensor_add(out=offset[name][:], in0=offset[name][:], in1=cols[name][:, 2, :])
+
+        def inv_col(name):
+            if name == "q":
+                return inv["qk"][:, 0:1]
+            if name == "k":
+                return inv["qk"][:, 1:2]
+            m = V_NAMES.index(name)
+            return inv["v"][:, m : m + 1]
+
+        upper, tall, v_pooled, v_turned, q_normed, q_turned = {}, {}, {}, {}, {}, {}
+        k_pooled = keep.tile([P, N_CHUNKS * POOLED], F32, name="k_pooled")
+        k_out = keep.tile([P, N_CHUNKS * POOLED], F32, name="k_out")
+
+        def by_row(c, name):
+            return acc[c, name][:].rearrange("ch (hp dh w) -> ch hp dh w", dh=2, w=WIDTH)
+
+        def scalar_part(c, name):
+            if name == "q":
+                q_normed[c] = work.tile([P, PACK, P], F32, name="q_normed")
+                nc.scalar.activation(
+                    out=q_normed[c][:],
+                    in_=acc[c, name][:].rearrange("ch (p i) -> ch i p", i=PACK),
+                    func=ACT.Identity,
+                    bias=offset["qk"][:, 0:1],
+                    scale=inv["qk"][:, 0:1],
+                )
+            else:
+                upper[c, name] = halves.tile([P, CHUNK // 2], F32, name="upper")
+                nc.scalar.activation(
+                    out=upper[c, name][:].rearrange("ch (hp w) -> ch hp w", w=WIDTH),
+                    in_=by_row(c, name)[:, :, 0, :], func=ACT.Copy, scale=inv_col(name),
+                )
+
+        def vector_part(c, name):
+            if name == "k":
+                tall[c, "k"] = work.tile([P, CHUNK // 2], F32, name="k_tall")
+                out = tall[c, "k"][:]
+            else:
+                if (c, "v") not in tall:
+                    tall[c, "v"] = work.tile([P, V_TILES, CHUNK // 2], F32, name="tall")
+                out = tall[c, "v"][:, V_NAMES.index(name), :]
             nc.vector.scalar_tensor_tensor(
                 out=out.rearrange("ch (hp w) -> ch hp w", w=WIDTH),
-                in0=by_row[:, :, 1, :],
-                scalar=inv_col,
-                in1=upper_rows,
+                in0=by_row(c, name)[:, :, 1, :],
+                scalar=inv_col(name),
+                in1=upper[c, name][:].rearrange("ch (hp w) -> ch hp w", w=WIDTH),
                 op0=ALU.mult,
                 op1=ALU.max,
             )
 
-        def pool_columns(tall, out):
-            pairs = tall.rearrange("ch (x dw) -> ch x dw", dw=2)
+        def pool_columns(tall_ap, out):
+            pairs = tall_ap.rearrange("ch (x dw) -> ch x dw", dw=2)
             nc.vector.tensor_tensor(out=out, in0=pairs[:, :, 0], in1=pairs[:, :, 1], op=ALU.max)
 
-        v_acc, v_pooled, v_turned, q_acc, k_acc, q_normed, q_turned = {}, {}, {}, {}, {}, {}, {}
-        norms = {}
-        k_pooled = keep.tile([P, N_CHUNKS * POOLED], F32, name="k_pooled")
-
-        def v_sums(c):
-            v_acc[c] = [convolve(c, wv, wv_planes, slice(m * P, (m + 1) * P)) for m in range(V_TILES)]
-
-        def v_leave(c):
-            inv = norms["v"][0]
-            tall = work.tile([P, V_TILES, CHUNK // 2], F32, name="tall")
-            for m in range(V_TILES):
-                pool_rows(v_acc[c][m], inv[:, m : m + 1], tall[:, m, :])
+        def v_pool(c):
             v_pooled[c] = work.tile([P, V_TILES * POOLED], F32, name="v_pooled")
-            pool_columns(tall[:].rearrange("ch m x -> ch (m x)"), v_pooled[c][:])
+            pool_columns(tall[c, "v"][:].rearrange("ch m x -> ch (m x)"), v_pooled[c][:])
 
         def v_turn(c):
             v_turned[c] = turned.tile([P, CV], F32, tag="turned", name="v_turned")
@@ -211,24 +257,6 @@ def tile_selfattention_pa_kernel(
             v_out = work.tile([P, CV], F32, name="v_out")
             nc.vector.tensor_tensor(out=v_out[:], in0=v_turned[c][:], in1=v_offset_rows[:], op=ALU.add)
             nc.sync.dma_start(out=out_2[0, c * POOLED : (c + 1) * POOLED, :], in_=v_out[:])
-
-        def qk_sums(c):
-            q_acc[c] = convolve(c, wq, wq_planes, slice(0, CQ))
-            k_acc[c] = convolve(c, wk, wk_planes, slice(0, CQ))
-
-        def qk_leave(c):
-            inv, offset = norms["qk"]
-            q_normed[c] = work.tile([P, PACK, P], F32, name="q_normed")
-            nc.scalar.activation(
-                out=q_normed[c][:],
-                in_=q_acc[c][:].rearrange("ch (p i) -> ch i p", i=PACK),
-                func=ACT.Identity,
-                bias=offset[:, 0:1],
-                scale=inv[:, 0:1],
-            )
-            k_tall = work.tile([P, CHUNK // 2], F32, name="k_tall")
-            pool_rows(k_acc[c], inv[:, 1:2], k_tall[:])
-            pool_columns(k_tall[:], k_pooled[:, c * POOLED : (c + 1) * POOLED])
 
         def q_turn(c):
             q_turned[c] = turned.tile([P, PACK, P], F32, tag="turned", name="q_turned")
@@ -243,43 +271,88 @@ def tile_selfattention_pa_kernel(
                 in_=q_out[:],
             )
 
-        v_stages = (v_sums, v_leave, v_turn, v_store)
-        qk_stages = (qk_sums, qk_leave, q_turn, q_store)
-        jobs = []
-        for c in range(N_CHUNKS + 1):
-            if c < N_CHUNKS:
-                jobs.append((v_stages, c))
-            if c >= 1:
-                jobs.append((qk_stages, c - 1))
+        def k_finish(c):
+            part = slice(c * POOLED, (c + 1) * POOLED)
+            pool_columns(tall[c, "k"][:], k_pooled[:, part])
+            nc.gpsimd.tensor_scalar(
+                out=k_out[:, part], in0=k_pooled[:, part], scalar1=1.0, scalar2=offset["qk"][:, 1:2],
+                op0=ALU.mult, op1=ALU.add,
+            )
+            nc.sync.dma_start(out=out_1[0][:, part], in_=k_out[:, part])
 
-        norms["v"] = batch_norm_columns(v_rows, V_TILES, "v")
-        norms["qk"] = batch_norm_columns(qk_rows, 2, "qk")
+        tiles = []
+        for kind, c in JOBS:
+            tiles.extend((c, name) for name in (V_NAMES if kind == "v" else ("q", "k")))
+
+        def scalar_part_of(t):
+            if t < len(tiles):
+                scalar_part(*tiles[t])
+
+        def multiply_tile(t):
+            if t < len(tiles):
+                multiply(tiles[t][0], tiles[t][1], range(PASSES))
+
+        regroup_vector(0, 0)
+        regroup_scalar(0, 0)
+        norm_turn(v_rows, V_TILES, "v")
+        norm_root("v")
+        regroup_vector(0, 1)
+        regroup_scalar(0, 1)
+        norm_finish("v")
+        for g in range(PASSES):
+            quantise(0, g)
+            for t in range(V_TILES):
+                multiply(tiles[t][0], tiles[t][1], (g,))
         v_offset_cols = keep.tile([P, V_TILES, P], F32, name="v_offset_cols")
-        nc.vector.tensor_copy(out=v_offset_cols[:], in_=norms["v"][1][:].unsqueeze(2).to_broadcast([P, V_TILES, P]))
+        nc.vector.tensor_copy(out=v_offset_cols[:], in_=offset["v"][:].unsqueeze(2).to_broadcast([P, V_TILES, P]))
         v_offset_rows = keep.tile([P, CV], F32, name="v_offset_rows")
         spread = turned.tile([P, CV], F32, tag="turned", name="spread")
         for m in range(V_TILES):
             nc.tensor.transpose(spread[:, m * P : (m + 1) * P], v_offset_cols[:, m, :], identity[:])
+        for g in range(PASSES):
+            regroup_vector(1, g)
+            regroup_scalar(1, g)
+        quantise(1, 0)
+        quantise(1, 1)
+        multiply_tile(4)
+        multiply_tile(5)
         nc.vector.tensor_copy(out=v_offset_rows[:], in_=spread[:])
-
-        quantise_chunk(0)
-        v_sums(0)
-        quantise_chunk(1)
-        v_sums(1)
-        for i, (stages, c) in enumerate(jobs):
-            start_sums, leave, turn, store = stages
-            leave(c)
-            if stages is v_stages and c + AHEAD < N_CHUNKS:
-                quantise_chunk(c + AHEAD)
-            turn(c)
-            for later_stages, later_c in jobs[i + AHEAD : i + AHEAD + 1]:
-                later_stages[0](later_c)
-            if i >= 1:
-                earlier_stages, earlier_c = jobs[i - 1]
-                earlier_stages[3](earlier_c)
-        last_stages, last_c = jobs[-1]
-        last_stages[3](last_c)
-
-        k_out = keep.tile([P, N_CHUNKS * POOLED], F32, name="k_out")
-        nc.vector.tensor_scalar_add(out=k_out[:], in0=k_pooled[:], scalar1=norms["qk"][1][:, 1:2])
-        nc.sync.dma_start(out=out_1[0], in_=k_out[:])
+        for t in range(LEAD):
+            scalar_part_of(t)
+        v_waiting, q_waiting = [], []
+        for t, (c, name) in enumerate(tiles):
+            scalar_part_of(t + LEAD)
+            if name != "q":
+                vector_part(c, name)
+            multiply_tile(t + BANKS)
+            if name == V_NAMES[-1]:
+                ahead = c + AHEAD
+                if ahead < N_CHUNKS:
+                    regroup_scalar(ahead, 0)
+                    regroup_scalar(ahead, 1)
+                    regroup_vector(ahead, 0)
+                    regroup_vector(ahead, 1)
+                v_pool(c)
+                v_turn(c)
+                if c == 0:
+                    norm_turn(qk_rows, 2, "qk")
+                    norm_root("qk")
+                for earlier in v_waiting:
+                    v_store(earlier)
+                v_waiting = [c]
+                if ahead < N_CHUNKS:
+                    quantise(ahead, 0)
+                    quantise(ahead, 1)
+                if c == 0:
+                    norm_finish("qk")
+            if name == "q":
+                q_turn(c)
+                for earlier in q_waiting:
+                    q_store(earlier)
+                q_waiting = [c]
+            if name == "k":
+                k_finish(c)
+        for c in v_waiting:
+            v_store(c)
+        for c in q_waiting:
+            q_store(c)

@@ -31,7 +31,7 @@ AHEAD = 2
 BANKS = 6
 LEAD = 2
 V_NAMES = ("v0", "v1", "v2", "v3")
-JOBS = (("v", 0), ("v", 1), ("q", 0), ("v", 2), ("q", 1), ("v", 3), ("q", 2), ("q", 3))
+JOBS = (("v", 0), ("v", 1), ("q", 0), ("q", 1), ("v", 2), ("q", 2), ("v", 3), ("q", 3))
 
 FLOPS = 2 * CH * POSITIONS * (CQ + CQ + CV)
 
@@ -170,25 +170,36 @@ def tile_selfattention_pa_kernel(
                     stop=(g == PASSES - 1),
                 )
 
-        cols, inv, offset = {}, {}, {}
+        cols_psum, cols, inv, offset, widths = {}, {}, {}, {}, {}
 
         def norm_turn(rows, n, name):
-            cols_psum = turned.tile([P, P], BF16, tag="turned", name=name + "_cols_psum")
-            nc.tensor.transpose(cols_psum[:], rows[:], identity_bf16[:])
+            cols_psum[name] = turned.tile([P, P], BF16, tag="turned", name=name + "_cols_psum")
+            nc.tensor.transpose(cols_psum[name][:], rows[:], identity_bf16[:])
+            widths[name] = n
             cols[name] = keep.tile([P, 5, n], F32, name=name + "_cols")
-            nc.vector.tensor_copy(out=cols[name][:], in_=cols_psum[:, 0 : 5 * n].rearrange("p (i m) -> p i m", m=n))
             inv[name] = keep.tile([P, n], F32, name=name + "_inv")
             offset[name] = keep.tile([P, n], F32, name=name + "_offset")
-            nc.vector.tensor_sub(out=offset[name][:], in0=cols[name][:, 0, :], in1=cols[name][:, 3, :])
 
         def norm_root(name):
             nc.scalar.activation(out=inv[name][:], in_=cols[name][:, 4, :], func=ACT.Sqrt, bias=eps_col[:], scale=1.0)
 
-        def norm_finish(name):
-            nc.vector.reciprocal(out=inv[name][:], in_=inv[name][:])
-            nc.vector.tensor_mul(out=inv[name][:], in0=inv[name][:], in1=cols[name][:, 1, :])
-            nc.vector.tensor_mul(out=offset[name][:], in0=offset[name][:], in1=inv[name][:])
-            nc.vector.tensor_add(out=offset[name][:], in0=offset[name][:], in1=cols[name][:, 2, :])
+        def norm_step(name, step):
+            bias, gain, shift, mean = [cols[name][:, i, :] for i in range(4)]
+            n = widths[name]
+            if step == "copy":
+                nc.vector.tensor_copy(
+                    out=cols[name][:], in_=cols_psum[name][:, 0 : 5 * n].rearrange("p (i m) -> p i m", m=n)
+                )
+            elif step == "difference":
+                nc.vector.tensor_sub(out=offset[name][:], in0=bias, in1=mean)
+            elif step == "reciprocal":
+                nc.vector.reciprocal(out=inv[name][:], in_=inv[name][:])
+            elif step == "inv":
+                nc.vector.tensor_mul(out=inv[name][:], in0=inv[name][:], in1=gain)
+            elif step == "product":
+                nc.vector.tensor_mul(out=offset[name][:], in0=offset[name][:], in1=inv[name][:])
+            else:
+                nc.vector.tensor_add(out=offset[name][:], in0=offset[name][:], in1=shift)
 
         def inv_col(name):
             if name == "q":
@@ -265,7 +276,10 @@ def tile_selfattention_pa_kernel(
 
         def q_store(c):
             q_out = work.tile([P, PACK, P], F32, name="q_out")
-            nc.scalar.copy(out=q_out[:], in_=q_turned[c][:])
+            if c == N_CHUNKS - 1:
+                nc.vector.tensor_copy(out=q_out[:], in_=q_turned[c][:])
+            else:
+                nc.scalar.copy(out=q_out[:], in_=q_turned[c][:])
             nc.sync.dma_start(
                 out=out_0[0, c * CHUNK : (c + 1) * CHUNK, :].rearrange("(p i) ch -> p i ch", i=PACK),
                 in_=q_out[:],
@@ -295,64 +309,100 @@ def tile_selfattention_pa_kernel(
         regroup_vector(0, 0)
         regroup_scalar(0, 0)
         norm_turn(v_rows, V_TILES, "v")
+        norm_step("v", "copy")
         norm_root("v")
         regroup_vector(0, 1)
         regroup_scalar(0, 1)
-        norm_finish("v")
-        for g in range(PASSES):
-            quantise(0, g)
-            for t in range(V_TILES):
-                multiply(tiles[t][0], tiles[t][1], (g,))
+        norm_step("v", "difference")
+        quantise(0, 0)
+        for t in range(V_TILES):
+            multiply(tiles[t][0], tiles[t][1], (0,))
+        norm_step("v", "reciprocal")
+        quantise(0, 1)
+        for t in range(V_TILES):
+            multiply(tiles[t][0], tiles[t][1], (1,))
+        norm_step("v", "inv")
+        regroup_vector(1, 0)
+        regroup_scalar(1, 0)
+        norm_step("v", "product")
+        regroup_vector(1, 1)
+        regroup_scalar(1, 1)
+        norm_step("v", "offset")
+        quantise(1, 0)
         v_offset_cols = keep.tile([P, V_TILES, P], F32, name="v_offset_cols")
         nc.vector.tensor_copy(out=v_offset_cols[:], in_=offset["v"][:].unsqueeze(2).to_broadcast([P, V_TILES, P]))
         v_offset_rows = keep.tile([P, CV], F32, name="v_offset_rows")
         spread = turned.tile([P, CV], F32, tag="turned", name="spread")
         for m in range(V_TILES):
             nc.tensor.transpose(spread[:, m * P : (m + 1) * P], v_offset_cols[:, m, :], identity[:])
-        for g in range(PASSES):
-            regroup_vector(1, g)
-            regroup_scalar(1, g)
-        quantise(1, 0)
+        norm_turn(qk_rows, 2, "qk")
         quantise(1, 1)
         multiply_tile(4)
         multiply_tile(5)
-        nc.vector.tensor_copy(out=v_offset_rows[:], in_=spread[:])
         for t in range(LEAD):
             scalar_part_of(t)
-        v_waiting, q_waiting = [], []
+
+        def spread_copy():
+            nc.vector.tensor_copy(out=v_offset_rows[:], in_=spread[:])
+
+        small = [("qk", "copy"), ("qk", "difference"), None, ("qk", "reciprocal"), ("qk", "inv"), ("qk", "product"), ("qk", "offset")]
+
+        progress = {"small": 0}
+
+        def one_small_step():
+            i = progress["small"]
+            if i < len(small):
+                progress["small"] = i + 1
+                if small[i] is None:
+                    spread_copy()
+                else:
+                    norm_step(*small[i])
+
+        v_waiting, q_waiting, k_waiting = [], [], []
         for t, (c, name) in enumerate(tiles):
             scalar_part_of(t + LEAD)
+            if t == 1:
+                norm_root("qk")
             if name != "q":
                 vector_part(c, name)
             multiply_tile(t + BANKS)
+            if name != "q":
+                for earlier in k_waiting:
+                    k_finish(earlier)
+                k_waiting = []
+                one_small_step()
             if name == V_NAMES[-1]:
                 ahead = c + AHEAD
                 if ahead < N_CHUNKS:
                     regroup_scalar(ahead, 0)
                     regroup_scalar(ahead, 1)
                     regroup_vector(ahead, 0)
+                    one_small_step()
                     regroup_vector(ahead, 1)
+                    one_small_step()
+                else:
+                    for earlier in v_waiting:
+                        v_store(earlier)
+                    v_waiting = []
                 v_pool(c)
                 v_turn(c)
-                if c == 0:
-                    norm_turn(qk_rows, 2, "qk")
-                    norm_root("qk")
+                one_small_step()
                 for earlier in v_waiting:
                     v_store(earlier)
                 v_waiting = [c]
                 if ahead < N_CHUNKS:
                     quantise(ahead, 0)
                     quantise(ahead, 1)
-                if c == 0:
-                    norm_finish("qk")
             if name == "q":
                 q_turn(c)
                 for earlier in q_waiting:
                     q_store(earlier)
                 q_waiting = [c]
             if name == "k":
-                k_finish(c)
+                k_waiting = [c]
         for c in v_waiting:
             v_store(c)
+        for c in k_waiting:
+            k_finish(c)
         for c in q_waiting:
             q_store(c)

@@ -276,10 +276,7 @@ def tile_selfattention_pa_kernel(
 
         def q_store(c):
             q_out = work.tile([P, PACK, P], F32, name="q_out")
-            if c == N_CHUNKS - 1:
-                nc.vector.tensor_copy(out=q_out[:], in_=q_turned[c][:])
-            else:
-                nc.scalar.copy(out=q_out[:], in_=q_turned[c][:])
+            nc.scalar.copy(out=q_out[:], in_=q_turned[c][:])
             nc.sync.dma_start(
                 out=out_0[0, c * CHUNK : (c + 1) * CHUNK, :].rearrange("(p i) ch -> p i ch", i=PACK),
                 in_=q_out[:],
@@ -384,6 +381,11 @@ def tile_selfattention_pa_kernel(
                     for earlier in v_waiting:
                         v_store(earlier)
                     v_waiting = []
+                if c == N_CHUNKS - 1:
+                    for earlier in q_waiting:
+                        q_store(earlier)
+                    q_turn(c)
+                    q_waiting = [c]
                 v_pool(c)
                 v_turn(c)
                 one_small_step()
@@ -394,15 +396,14 @@ def tile_selfattention_pa_kernel(
                     quantise(ahead, 0)
                     quantise(ahead, 1)
             if name == "q":
-                q_turn(c)
+                if c < N_CHUNKS - 1:
+                    q_turn(c)
                 for earlier in q_waiting:
                     q_store(earlier)
-                q_waiting = [c]
+                q_waiting = [c] if c < N_CHUNKS - 1 else []
             if name == "k":
                 k_waiting = [c]
-        for c in v_waiting:
-            v_store(c)
         for c in k_waiting:
             k_finish(c)
-        for c in q_waiting:
-            q_store(c)
+        for c in v_waiting:
+            v_store(c)

@@ -27,11 +27,17 @@ V_TILES = CV // P
 QUADRANTS = 4
 RUN = 4
 VECTOR_COLS = 256
-AHEAD = 2
 BANKS = 6
 LEAD = 2
 V_NAMES = ("v0", "v1", "v2", "v3")
 JOBS = (("v", 0), ("v", 1), ("q", 0), ("q", 1), ("v", 2), ("q", 2), ("v", 3), ("q", 3))
+SCALAR_REGROUPS = (-4, -3)
+VECTOR_REGROUPS = (-2, -1)
+POOL_LATER = 2
+V_STORE_LATER = 5
+Q_TURN_LATER = 1
+Q_STORE_LATER = 3
+K_FINISH_LATER = 1
 
 FLOPS = 2 * CH * POSITIONS * (CQ + CQ + CV)
 
@@ -294,14 +300,46 @@ def tile_selfattention_pa_kernel(
         tiles = []
         for kind, c in JOBS:
             tiles.extend((c, name) for name in (V_NAMES if kind == "v" else ("q", "k")))
+        n_tiles = len(tiles)
+        last_v = tiles.index((N_CHUNKS - 1, V_NAMES[-1]))
 
-        def scalar_part_of(t):
-            if t < len(tiles):
-                scalar_part(*tiles[t])
+        plan = {}
 
-        def multiply_tile(t):
-            if t < len(tiles):
+        def at(t, place, step, *args):
+            plan.setdefault((max(t, 0), place), []).append((step, args))
+
+        def run(t, place):
+            for step, args in plan.get((t, place), []):
+                step(*args)
+
+        for c in range(2, N_CHUNKS):
+            due = min(t for t in range(n_tiles) if tiles[t][0] == c) - BANKS
+            for g in range(PASSES):
+                at(due + SCALAR_REGROUPS[g], "scalar", regroup_scalar, c, g)
+                at(due + VECTOR_REGROUPS[g], "vector", regroup_vector, c, g)
+                at(due, "quantise", quantise, c, g)
+        for t, (c, name) in enumerate(tiles):
+            if c == N_CHUNKS - 1:
+                continue
+            if name == V_NAMES[-1]:
+                at(t + POOL_LATER, "turn", v_pool, c)
+                at(t + POOL_LATER, "turn", v_turn, c)
+                if c < N_CHUNKS - 2:
+                    at(t + POOL_LATER + V_STORE_LATER, "end", v_store, c)
+            if name == "q":
+                at(t + Q_TURN_LATER, "turn", q_turn, c)
+                at(min(t + Q_TURN_LATER + Q_STORE_LATER, last_v), "end", q_store, c)
+            if name == "k":
+                at(min(t + K_FINISH_LATER, last_v), "end", k_finish, c)
+
+        quantised = set()
+        progress = {"small": 0, "multiplied": 0}
+
+        def multiply_ready_tiles(left):
+            while progress["multiplied"] < min(n_tiles, left + BANKS) and tiles[progress["multiplied"]][0] in quantised:
+                t = progress["multiplied"]
                 multiply(tiles[t][0], tiles[t][1], range(PASSES))
+                progress["multiplied"] = t + 1
 
         regroup_vector(0, 0)
         regroup_scalar(0, 0)
@@ -334,17 +372,17 @@ def tile_selfattention_pa_kernel(
             nc.tensor.transpose(spread[:, m * P : (m + 1) * P], v_offset_cols[:, m, :], identity[:])
         norm_turn(qk_rows, 2, "qk")
         quantise(1, 1)
-        multiply_tile(4)
-        multiply_tile(5)
+        quantised.add(0)
+        quantised.add(1)
+        progress["multiplied"] = V_TILES
+        multiply_ready_tiles(0)
         for t in range(LEAD):
-            scalar_part_of(t)
+            scalar_part(*tiles[t])
 
         def spread_copy():
             nc.vector.tensor_copy(out=v_offset_rows[:], in_=spread[:])
 
         small = [("qk", "copy"), ("qk", "difference"), None, ("qk", "reciprocal"), ("qk", "inv"), ("qk", "product"), ("qk", "offset")]
-
-        progress = {"small": 0}
 
         def one_small_step():
             i = progress["small"]
@@ -354,56 +392,33 @@ def tile_selfattention_pa_kernel(
                     spread_copy()
                 else:
                     norm_step(*small[i])
+                    if small[i][1] == "copy":
+                        norm_root("qk")
 
-        v_waiting, q_waiting, k_waiting = [], [], []
         for t, (c, name) in enumerate(tiles):
-            scalar_part_of(t + LEAD)
-            if t == 1:
-                norm_root("qk")
+            if t + LEAD < n_tiles:
+                scalar_part(*tiles[t + LEAD])
+            run(t, "scalar")
+            if (c, name) == (N_CHUNKS - 1, "q"):
+                break
             if name != "q":
                 vector_part(c, name)
-            multiply_tile(t + BANKS)
-            if name != "q":
-                for earlier in k_waiting:
-                    k_finish(earlier)
-                k_waiting = []
+            one_small_step()
+            for step, args in plan.get((t, "vector"), []):
+                step(*args)
                 one_small_step()
-            if name == V_NAMES[-1]:
-                ahead = c + AHEAD
-                if ahead < N_CHUNKS:
-                    regroup_scalar(ahead, 0)
-                    regroup_scalar(ahead, 1)
-                    regroup_vector(ahead, 0)
-                    one_small_step()
-                    regroup_vector(ahead, 1)
-                    one_small_step()
-                else:
-                    for earlier in v_waiting:
-                        v_store(earlier)
-                    v_waiting = []
-                if c == N_CHUNKS - 1:
-                    for earlier in q_waiting:
-                        q_store(earlier)
-                    q_turn(c)
-                    q_waiting = [c]
-                v_pool(c)
-                v_turn(c)
-                one_small_step()
-                for earlier in v_waiting:
-                    v_store(earlier)
-                v_waiting = [c]
-                if ahead < N_CHUNKS:
-                    quantise(ahead, 0)
-                    quantise(ahead, 1)
-            if name == "q":
-                if c < N_CHUNKS - 1:
-                    q_turn(c)
-                for earlier in q_waiting:
-                    q_store(earlier)
-                q_waiting = [c] if c < N_CHUNKS - 1 else []
-            if name == "k":
-                k_waiting = [c]
-        for c in k_waiting:
-            k_finish(c)
-        for c in v_waiting:
-            v_store(c)
+            for step, args in plan.get((t, "quantise"), []):
+                step(*args)
+                quantised.add(args[0])
+            multiply_ready_tiles(t + 1)
+            run(t, "turn")
+            run(t, "end")
+        last = N_CHUNKS - 1
+        v_store(last - 1)
+        q_turn(last)
+        v_pool(last)
+        v_turn(last)
+        q_store(last)
+        vector_part(last, "k")
+        k_finish(last)
+        v_store(last)

@@ -25,7 +25,7 @@ N_CHUNKS = POSITIONS // CHUNK
 POOLED = CHUNK // 4
 V_TILES = CV // P
 QUADRANTS = 4
-RUN = 4
+RUN = 8
 VECTOR_COLS = 256
 BANKS = 6
 LEAD = 2

@@ -197,15 +197,15 @@ def tile_selfattention_pa_kernel(
                     out=cols[name][:], in_=cols_psum[name][:, 0 : 5 * n].rearrange("p (i m) -> p i m", m=n)
                 )
             elif step == "difference":
-                nc.vector.tensor_sub(out=offset[name][:], in0=bias, in1=mean)
+                nc.gpsimd.tensor_tensor(out=offset[name][:], in0=bias, in1=mean, op=ALU.subtract)
             elif step == "reciprocal":
                 nc.vector.reciprocal(out=inv[name][:], in_=inv[name][:])
             elif step == "inv":
-                nc.vector.tensor_mul(out=inv[name][:], in0=inv[name][:], in1=gain)
+                nc.gpsimd.tensor_tensor(out=inv[name][:], in0=inv[name][:], in1=gain, op=ALU.mult)
             elif step == "product":
-                nc.vector.tensor_mul(out=offset[name][:], in0=offset[name][:], in1=inv[name][:])
+                nc.gpsimd.tensor_tensor(out=offset[name][:], in0=offset[name][:], in1=inv[name][:], op=ALU.mult)
             else:
-                nc.vector.tensor_add(out=offset[name][:], in0=offset[name][:], in1=shift)
+                nc.gpsimd.tensor_tensor(out=offset[name][:], in0=offset[name][:], in1=shift, op=ALU.add)
 
         def inv_col(name):
             if name == "q":
@@ -365,7 +365,7 @@ def tile_selfattention_pa_kernel(
         norm_step("v", "offset")
         quantise(1, 0)
         v_offset_cols = keep.tile([P, V_TILES, P], F32, name="v_offset_cols")
-        nc.vector.tensor_copy(out=v_offset_cols[:], in_=offset["v"][:].unsqueeze(2).to_broadcast([P, V_TILES, P]))
+        nc.gpsimd.tensor_copy(out=v_offset_cols[:], in_=offset["v"][:].unsqueeze(2).to_broadcast([P, V_TILES, P]))
         v_offset_rows = keep.tile([P, CV], F32, name="v_offset_rows")
         spread = turned.tile([P, CV], F32, tag="turned", name="spread")
         for m in range(V_TILES):
@@ -380,7 +380,7 @@ def tile_selfattention_pa_kernel(
             scalar_part(*tiles[t])
 
         def spread_copy():
-            nc.vector.tensor_copy(out=v_offset_rows[:], in_=spread[:])
+            nc.scalar.copy(out=v_offset_rows[:], in_=spread[:])
 
         small = [("qk", "copy"), ("qk", "difference"), None, ("qk", "reciprocal"), ("qk", "inv"), ("qk", "product"), ("qk", "offset")]
 

from contextlib import ExitStack

import concourse.mybir as mybir
from concourse.masks import make_identity

F32 = mybir.dt.float32
BF16 = mybir.dt.bfloat16
I32 = mybir.dt.int32
U32 = mybir.dt.uint32
U8 = mybir.dt.uint8
FP8X4 = mybir.dt.float8_e4m3fn_x4
ALU = mybir.AluOpType
ACT = mybir.ActivationFunctionType

P = 128
PACK = 4
K_PASS = P * PACK
CH, CQ, CV = 1024, 128, 512
HEIGHT, WIDTH = 32, 64
POSITIONS = HEIGHT * WIDTH
EPS = 1e-5
PASSES = CH // K_PASS
CHUNK = 512
N_CHUNKS = POSITIONS // CHUNK
POOLED = CHUNK // 4
V_TILES = CV // P
QUADRANTS = 4
RUN = 8
VECTOR_COLS = 256
BANKS = 6
LEAD = 2
V_NAMES = ("v0", "v1", "v2", "v3")
JOBS = (("v", 0), ("v", 1), ("q", 0), ("q", 1), ("v", 2), ("q", 2), ("v", 3), ("q", 3))
SCALAR_REGROUPS = (-4, -3)
VECTOR_REGROUPS = (-2, -1)
POOL_LATER = 2
V_STORE_LATER = 5
Q_TURN_LATER = 1
Q_STORE_LATER = 3
K_FINISH_LATER = 1

FLOPS = 2 * CH * POSITIONS * (CQ + CQ + CV)


def weight_tiles(nc, keep, words_dram, scales_dram, n_out, name):
    words = keep.tile([P, PASSES, n_out], U32, name=name + "_words", align_bytes=64)
    loads = [(words[:].bitcast(I32), words_dram.rearrange("g p n t -> p g (n t)").bitcast(I32))]
    planes = keep.tile([P, PASSES, n_out], U8, name=name + "_planes", align_bytes=64)
    nc.vector.memset(planes[:].bitcast(I32), 0)
    for quad in range(QUADRANTS):
        loads.append(
            (
                planes[32 * quad : 32 * quad + 4].bitcast(I32),
                scales_dram[:, 4 * quad : 4 * quad + 4, :].rearrange("g r n -> r g n").bitcast(I32),
            )
        )
    return words, planes, loads


def vector_rows(nc, keep, groups, name):
    rows = keep.tile([P, P], BF16, name=name + "_rows")
    nc.gpsimd.memset(rows[:], 0.0)
    loads = []
    row = 0
    for vectors in groups:
        for vector in vectors:
            n_rows = vector.shape[0] // P
            loads.append((rows[row : row + n_rows, :], vector.rearrange("(m c) -> m c", c=P)))
            row += n_rows
    return rows, loads


def tile_selfattention_pa_kernel(
    tc,
    memory,
    wq_words, wq_scales, bq, bnq_s, bnq_b, bnq_m, bnq_v,
    wk_words, wk_scales, bk, bnk_s, bnk_b, bnk_m, bnk_v,
    wv_words, wv_scales, bv, bnv_s, bnv_b, bnv_m, bnv_v,
    out_0, out_1, out_2,
):
    nc = tc.nc
    mem_rows = memory.rearrange("b (g p j) h w -> (b g) p j (h w)", p=P, j=PACK)

    with ExitStack() as ctx:
        keep = ctx.enter_context(tc.tile_pool(name="keep", bufs=1))
        raw_pool = ctx.enter_context(tc.tile_pool(name="raw", bufs=N_CHUNKS * PASSES))
        grouped_pool = ctx.enter_context(tc.tile_pool(name="grouped", bufs=4))
        work = ctx.enter_context(tc.tile_pool(name="work", bufs=2))
        halves = ctx.enter_context(tc.tile_pool(name="halves", bufs=4))
        sums = ctx.enter_context(tc.psum_pool(name="sums", bufs=6))
        turned = ctx.enter_context(tc.psum_pool(name="turned", bufs=2))
        ctx.enter_context(tc.manual_schedule())

        eps_col = keep.tile([P, 1], F32, name="eps_col")
        nc.vector.memset(eps_col[:], EPS)

        v_rows, v_row_loads = vector_rows(nc, keep, ((bv,), (bnv_s,), (bnv_b,), (bnv_m,), (bnv_v,)), "v")
        qk_rows, qk_row_loads = vector_rows(
            nc, keep, ((bq, bk), (bnq_s, bnk_s), (bnq_b, bnk_b), (bnq_m, bnk_m), (bnq_v, bnk_v)), "qk"
        )
        wv, wv_planes, wv_loads = weight_tiles(nc, keep, wv_words, wv_scales, CV, "wv")
        wq, wq_planes, wq_loads = weight_tiles(nc, keep, wq_words, wq_scales, CQ, "wq")
        wk, wk_planes, wk_loads = weight_tiles(nc, keep, wk_words, wk_scales, CQ, "wk")
        raw = {}

        def load_piece(c, g):
            raw[c, g] = raw_pool.tile([P, PACK, CHUNK], BF16, name="raw")
            nc.sync.dma_start(out=raw[c, g][:], in_=mem_rows[g][:, :, c * CHUNK : (c + 1) * CHUNK])

        def load_small(loads):
            for out, in_ in loads:
                nc.sync.dma_start(out=out, in_=in_)

        load_piece(0, 0)
        load_small(v_row_loads)
        load_piece(0, 1)
        load_small(wv_loads)
        load_piece(1, 0)
        load_piece(1, 1)
        load_small(qk_row_loads)
        load_piece(2, 0)
        load_piece(2, 1)
        load_small(wq_loads[:1] + wk_loads[:1] + wq_loads[1:] + wk_loads[1:])
        load_piece(3, 0)
        load_piece(3, 1)

        warm = keep.tile([P, 1], F32, name="warm")
        nc.scalar.activation(out=warm[:], in_=eps_col[:], func=ACT.Sqrt)
        identity_bf16 = keep.tile([P, P], BF16, name="identity_bf16")
        make_identity(nc, identity_bf16[:])
        identity = keep.tile([P, P], F32, name="identity")
        make_identity(nc, identity[:])

        mem_codes = keep.tile([P, N_CHUNKS, PASSES, CHUNK], U32, name="mem_codes", align_bytes=64)
        mem_planes = keep.tile([P, N_CHUNKS, PASSES, CHUNK], U8, name="mem_planes", align_bytes=64)
        grouped = {}

        def regroup(copy, cols, c, g):
            if (c, g) not in grouped:
                grouped[c, g] = grouped_pool.tile([P, CHUNK, PACK], BF16, name="grouped", align_bytes=64)
            copy(
                out=grouped[c, g][:, cols, :].rearrange("p (n i) j -> p n j i", i=RUN),
                in_=raw[c, g][:, :, cols].rearrange("p j (n i) -> p n j i", i=RUN),
            )

        def regroup_vector(c, g):
            regroup(nc.vector.tensor_copy, slice(0, VECTOR_COLS), c, g)

        def regroup_scalar(c, g):
            regroup(nc.scalar.copy, slice(VECTOR_COLS, CHUNK), c, g)

        def quantise(c, g):
            nc.vector.quantize_mx(
                out=mem_codes[:, c, g, :].bitcast(FP8X4),
                scales=mem_planes[:, c, g, :],
                in_=grouped[c, g][:].rearrange("p n j -> p (n j)"),
            )

        weights = {"q": (wq, wq_planes, slice(0, CQ)), "k": (wk, wk_planes, slice(0, CQ))}
        for m in range(V_TILES):
            weights["v%d" % m] = (wv, wv_planes, slice(m * P, (m + 1) * P))
        acc = {}

        def multiply(c, name, passes):
            if (c, name) not in acc:
                acc[c, name] = sums.tile([P, CHUNK], F32, name="acc")
            words, planes, channels = weights[name]
            for g in passes:
                nc.tensor.matmul_mx(
                    out=acc[c, name][:],
                    lhsT=words[:, g, channels].bitcast(FP8X4),
                    lhsT_scale=planes[:, g, channels],
                    rhs=mem_codes[:, c, g, :].bitcast(FP8X4),
                    rhs_scale=mem_planes[:, c, g, :],
                    start=(g == 0),
                    stop=(g == PASSES - 1),
                )

        cols_psum, cols, inv, offset, widths = {}, {}, {}, {}, {}

        def norm_turn(rows, n, name):
            cols_psum[name] = turned.tile([P, P], BF16, tag="turned", name=name + "_cols_psum")
            nc.tensor.transpose(cols_psum[name][:], rows[:], identity_bf16[:])
            widths[name] = n
            cols[name] = keep.tile([P, 5, n], F32, name=name + "_cols")
            inv[name] = keep.tile([P, n], F32, name=name + "_inv")
            offset[name] = keep.tile([P, n], F32, name=name + "_offset")

        def norm_root(name):
            nc.scalar.activation(out=inv[name][:], in_=cols[name][:, 4, :], func=ACT.Sqrt, bias=eps_col[:], scale=1.0)

        def norm_step(name, step):
            bias, gain, shift, mean = [cols[name][:, i, :] for i in range(4)]
            n = widths[name]
            if step == "copy":
                nc.vector.tensor_copy(
                    out=cols[name][:], in_=cols_psum[name][:, 0 : 5 * n].rearrange("p (i m) -> p i m", m=n)
                )
            elif step == "difference":
                nc.gpsimd.tensor_tensor(out=offset[name][:], in0=bias, in1=mean, op=ALU.subtract)
            elif step == "reciprocal":
                nc.vector.reciprocal(out=inv[name][:], in_=inv[name][:])
            elif step == "inv":
                nc.gpsimd.tensor_tensor(out=inv[name][:], in0=inv[name][:], in1=gain, op=ALU.mult)
            elif step == "product":
                nc.gpsimd.tensor_tensor(out=offset[name][:], in0=offset[name][:], in1=inv[name][:], op=ALU.mult)
            else:
                nc.gpsimd.tensor_tensor(out=offset[name][:], in0=offset[name][:], in1=shift, op=ALU.add)

        def inv_col(name):
            if name == "q":
                return inv["qk"][:, 0:1]
            if name == "k":
                return inv["qk"][:, 1:2]
            m = V_NAMES.index(name)
            return inv["v"][:, m : m + 1]

        upper, tall, v_pooled, v_turned, q_normed, q_turned = {}, {}, {}, {}, {}, {}
        k_pooled = keep.tile([P, N_CHUNKS * POOLED], F32, name="k_pooled")
        k_out = keep.tile([P, N_CHUNKS * POOLED], F32, name="k_out")

        def by_row(c, name):
            return acc[c, name][:].rearrange("ch (hp dh w) -> ch hp dh w", dh=2, w=WIDTH)

        def scalar_part(c, name):
            if name == "q":
                q_normed[c] = work.tile([P, PACK, P], F32, name="q_normed")
                nc.scalar.activation(
                    out=q_normed[c][:],
                    in_=acc[c, name][:].rearrange("ch (p i) -> ch i p", i=PACK),
                    func=ACT.Identity,
                    bias=offset["qk"][:, 0:1],
                    scale=inv["qk"][:, 0:1],
                )
            else:
                upper[c, name] = halves.tile([P, CHUNK // 2], F32, name="upper")
                nc.scalar.activation(
                    out=upper[c, name][:].rearrange("ch (hp w) -> ch hp w", w=WIDTH),
                    in_=by_row(c, name)[:, :, 0, :], func=ACT.Copy, scale=inv_col(name),
                )

        def vector_part(c, name):
            if name == "k":
                tall[c, "k"] = work.tile([P, CHUNK // 2], F32, name="k_tall")
                out = tall[c, "k"][:]
            else:
                if (c, "v") not in tall:
                    tall[c, "v"] = work.tile([P, V_TILES, CHUNK // 2], F32, name="tall")
                out = tall[c, "v"][:, V_NAMES.index(name), :]
            nc.vector.scalar_tensor_tensor(
                out=out.rearrange("ch (hp w) -> ch hp w", w=WIDTH),
                in0=by_row(c, name)[:, :, 1, :],
                scalar=inv_col(name),
                in1=upper[c, name][:].rearrange("ch (hp w) -> ch hp w", w=WIDTH),
                op0=ALU.mult,
                op1=ALU.max,
            )

        def pool_columns(tall_ap, out):
            pairs = tall_ap.rearrange("ch (x dw) -> ch x dw", dw=2)
            nc.vector.tensor_tensor(out=out, in0=pairs[:, :, 0], in1=pairs[:, :, 1], op=ALU.max)

        def v_pool(c):
            v_pooled[c] = work.tile([P, V_TILES * POOLED], F32, name="v_pooled")
            pool_columns(tall[c, "v"][:].rearrange("ch m x -> ch (m x)"), v_pooled[c][:])

        def v_turn(c):
            v_turned[c] = turned.tile([P, CV], F32, tag="turned", name="v_turned")
            for m in range(V_TILES):
                block = slice(m * P, (m + 1) * P)
                nc.tensor.transpose(v_turned[c][:, block], v_pooled[c][:, block], identity[:])

        def v_store(c):
            v_out = work.tile([P, CV], F32, name="v_out")
            nc.vector.tensor_tensor(out=v_out[:], in0=v_turned[c][:], in1=v_offset_rows[:], op=ALU.add)
            nc.sync.dma_start(out=out_2[0, c * POOLED : (c + 1) * POOLED, :], in_=v_out[:])

        def q_turn(c):
            q_turned[c] = turned.tile([P, PACK, P], F32, tag="turned", name="q_turned")
            for i in range(PACK):
                nc.tensor.transpose(q_turned[c][:, i, :], q_normed[c][:, i, :], identity[:])

        def q_store(c):
            q_out = work.tile([P, PACK, P], F32, name="q_out")
            nc.scalar.copy(out=q_out[:], in_=q_turned[c][:])
            nc.sync.dma_start(
                out=out_0[0, c * CHUNK : (c + 1) * CHUNK, :].rearrange("(p i) ch -> p i ch", i=PACK),
                in_=q_out[:],
            )

        def k_finish(c):
            part = slice(c * POOLED, (c + 1) * POOLED)
            pool_columns(tall[c, "k"][:], k_pooled[:, part])
            nc.gpsimd.tensor_scalar(
                out=k_out[:, part], in0=k_pooled[:, part], scalar1=1.0, scalar2=offset["qk"][:, 1:2],
                op0=ALU.mult, op1=ALU.add,
            )
            nc.sync.dma_start(out=out_1[0][:, part], in_=k_out[:, part])

        tiles = []
        for kind, c in JOBS:
            tiles.extend((c, name) for name in (V_NAMES if kind == "v" else ("q", "k")))
        n_tiles = len(tiles)
        last_v = tiles.index((N_CHUNKS - 1, V_NAMES[-1]))

        plan = {}

        def at(t, place, step, *args):
            plan.setdefault((max(t, 0), place), []).append((step, args))

        def run(t, place):
            for step, args in plan.get((t, place), []):
                step(*args)

        for c in range(2, N_CHUNKS):
            due = min(t for t in range(n_tiles) if tiles[t][0] == c) - BANKS
            for g in range(PASSES):
                at(due + SCALAR_REGROUPS[g], "scalar", regroup_scalar, c, g)
                at(due + VECTOR_REGROUPS[g], "vector", regroup_vector, c, g)
                at(due, "quantise", quantise, c, g)
        for t, (c, name) in enumerate(tiles):
            if c == N_CHUNKS - 1:
                continue
            if name == V_NAMES[-1]:
                at(t + POOL_LATER, "turn", v_pool, c)
                at(t + POOL_LATER, "turn", v_turn, c)
                if c < N_CHUNKS - 2:
                    at(t + POOL_LATER + V_STORE_LATER, "end", v_store, c)
            if name == "q":
                at(t + Q_TURN_LATER, "turn", q_turn, c)
                at(min(t + Q_TURN_LATER + Q_STORE_LATER, last_v), "end", q_store, c)
            if name == "k":
                at(min(t + K_FINISH_LATER, last_v), "end", k_finish, c)

        quantised = set()
        progress = {"small": 0, "multiplied": 0}

        def multiply_ready_tiles(left):
            while progress["multiplied"] < min(n_tiles, left + BANKS) and tiles[progress["multiplied"]][0] in quantised:
                t = progress["multiplied"]
                multiply(tiles[t][0], tiles[t][1], range(PASSES))
                progress["multiplied"] = t + 1

        regroup_vector(0, 0)
        regroup_scalar(0, 0)
        norm_turn(v_rows, V_TILES, "v")
        norm_step("v", "copy")
        norm_root("v")
        regroup_vector(0, 1)
        regroup_scalar(0, 1)
        norm_step("v", "difference")
        quantise(0, 0)
        for t in range(V_TILES):
            multiply(tiles[t][0], tiles[t][1], (0,))
        norm_step("v", "reciprocal")
        quantise(0, 1)
        for t in range(V_TILES):
            multiply(tiles[t][0], tiles[t][1], (1,))
        norm_step("v", "inv")
        regroup_vector(1, 0)
        regroup_scalar(1, 0)
        norm_step("v", "product")
        regroup_vector(1, 1)
        regroup_scalar(1, 1)
        norm_step("v", "offset")
        quantise(1, 0)
        v_offset_cols = keep.tile([P, V_TILES, P], F32, name="v_offset_cols")
        nc.gpsimd.tensor_copy(out=v_offset_cols[:], in_=offset["v"][:].unsqueeze(2).to_broadcast([P, V_TILES, P]))
        v_offset_rows = keep.tile([P, CV], F32, name="v_offset_rows")
        spread = turned.tile([P, CV], F32, tag="turned", name="spread")
        for m in range(V_TILES):
            nc.tensor.transpose(spread[:, m * P : (m + 1) * P], v_offset_cols[:, m, :], identity[:])
        norm_turn(qk_rows, 2, "qk")
        quantise(1, 1)
        quantised.add(0)
        quantised.add(1)
        progress["multiplied"] = V_TILES
        multiply_ready_tiles(0)
        for t in range(LEAD):
            scalar_part(*tiles[t])

        def spread_copy():
            nc.scalar.copy(out=v_offset_rows[:], in_=spread[:])

        small = [("qk", "copy"), ("qk", "difference"), None, ("qk", "reciprocal"), ("qk", "inv"), ("qk", "product"), ("qk", "offset")]

        def one_small_step():
            i = progress["small"]
            if i < len(small):
                progress["small"] = i + 1
                if small[i] is None:
                    spread_copy()
                else:
                    norm_step(*small[i])
                    if small[i][1] == "copy":
                        norm_root("qk")

        for t, (c, name) in enumerate(tiles):
            if t + LEAD < n_tiles:
                scalar_part(*tiles[t + LEAD])
            run(t, "scalar")
            if (c, name) == (N_CHUNKS - 1, "q"):
                break
            if name != "q":
                vector_part(c, name)
            one_small_step()
            for step, args in plan.get((t, "vector"), []):
                step(*args)
                one_small_step()
            for step, args in plan.get((t, "quantise"), []):
                step(*args)
                quantised.add(args[0])
            multiply_ready_tiles(t + 1)
            run(t, "turn")
            run(t, "end")
        last = N_CHUNKS - 1
        v_store(last - 1)
        q_turn(last)
        v_pool(last)
        v_turn(last)
        q_store(last)
        vector_part(last, "k")
        k_finish(last)
        v_store(last)
